import numpy as np
import ml_dtypes


def mxq(x, axis, fmt="e4m3"):
    dtype, down = {"e4m3": (ml_dtypes.float8_e4m3fn, 7), "e5m2": (ml_dtypes.float8_e5m2, 14)}[fmt]
    v = np.moveaxis(np.asarray(x, np.float32).astype(ml_dtypes.bfloat16).astype(np.float64), axis, -1)
    blocks = v.reshape(v.shape[:-1] + (-1, 32))
    amax = np.abs(blocks).max(-1, keepdims=True)
    byte = np.maximum(np.where(amax > 0, np.frexp(amax)[1] - 1 + 127, 0) - down, 1)
    scale = np.exp2(byte - 127.0)
    codes = (blocks / scale).astype(np.float32).astype(dtype).astype(np.float64)
    return np.moveaxis((codes * scale).reshape(v.shape), -1, axis)


WIDE = False


def mx_kscale(k):
    if not WIDE:
        return np.ones(k)
    levels = np.array([10, -10, 5, -5, 0])
    a = np.random.permutation(np.resize(levels, k // 512 * 4)).reshape(k // 512, 4)
    idx = np.arange(k)
    return np.exp2(a[idx // 512, idx % 128 // 32])


BF16 = ml_dtypes.bfloat16


def bf(x):
    return np.asarray(x, np.float32).astype(BF16)


def f64(x):
    return np.asarray(x).astype(np.float64)


B, Tq, Tk, C = 2, 2048, 512, 512
BETA = 2.35


def softplus(v):
    return np.log(1.0 + np.exp(v))


def setup_inputs():
    s = mx_kscale(C)
    level = np.random.standard_normal((B, Tk))[..., None]
    return {"q": bf(np.random.standard_normal((B, Tq, C)) * 1.5 * s),
            "k_mu": bf(np.random.standard_normal((B, Tk, C)) / s),
            "k_var": bf(softplus(np.random.standard_normal((B, Tk, C)) + level) / s / s),
            "v_sample": bf(np.random.standard_normal((B, Tk, C)) * 1.3)}


def reference(q, k_mu, k_var, v_sample):
    mean_scores = (mxq(f64(q), 2, "e4m3") @ mxq(f64(k_mu), 2, "e4m3").transpose(0, 2, 1)) / np.sqrt(C)
    q2 = f64(q) * f64(q)
    var_penalty = (mxq(q2, 2, "e4m3") @ mxq(f64(k_var), 2, "e4m3").transpose(0, 2, 1)) / C
    scores = mean_scores - BETA * np.sqrt(var_penalty)
    e = np.exp(scores - scores.max(-1, keepdims=True))
    return (mxq(e, 2, "e4m3") @ mxq(f64(v_sample), 1, "e4m3")) / e.sum(-1, keepdims=True)

@@ -1,0 +1,295 @@
+from contextlib import ExitStack
+import math
+
+import concourse.mybir as mybir
+from concourse.masks import make_identity
+
+F32 = mybir.dt.float32
+BF16 = mybir.dt.bfloat16
+U32 = mybir.dt.uint32
+U8 = mybir.dt.uint8
+FP8X4 = mybir.dt.float8_e4m3fn_x4
+FUNC = mybir.ActivationFunctionType
+ALU = mybir.AluOpType
+AXIS = mybir.AxisListType
+
+BATCH, TQ, TK, C = 2, 2048, 512, 512
+BETA = 2.35
+FLOPS = 3 * 2 * BATCH * TQ * TK * C
+
+P = 128
+PACK = 4
+HALVES = 2
+WORDS = C // 2
+PAIR = 2
+KEY_TILES = TK // P
+Q_TILES = TQ // P
+PAIRS_PER_BATCH = Q_TILES // PAIR
+N_PAIRS = BATCH * PAIRS_PER_BATCH
+LOAD_TILES = 4
+
+VALUES_AT = 3
+NEXT_KEYS_AT = 5
+
+
+def tile_probcrossattention_pb_t_kernel(tc, q, k_mu, k_var, v_sample, out):
+    nc = tc.nc
+    with ExitStack() as ctx:
+        ctx.enter_context(tc.manual_schedule())
+
+        const = ctx.enter_context(tc.tile_pool(name="const", bufs=1))
+        inputs = ctx.enter_context(tc.tile_pool(name="inputs", bufs=1))
+        keep = ctx.enter_context(tc.tile_pool(name="keep", bufs=1))
+        kv_stage = ctx.enter_context(tc.tile_pool(name="kv_stage", bufs=2))
+        q_stage = ctx.enter_context(tc.tile_pool(name="q_stage", bufs=3))
+        pen_stage = ctx.enter_context(tc.tile_pool(name="pen_stage", bufs=4))
+        e_stage = ctx.enter_context(tc.tile_pool(name="e_stage", bufs=3))
+        out_stage = ctx.enter_context(tc.tile_pool(name="out_stage", bufs=4))
+        psum_turn = ctx.enter_context(tc.psum_pool(name="psum_turn", bufs=2))
+        psum_acc = ctx.enter_context(tc.psum_pool(name="psum_acc", bufs=6))
+
+        ident_f32 = const.tile([P, P], F32)
+        make_identity(nc, ident_f32[:])
+        ident_bf16 = const.tile([P, P], BF16)
+        make_identity(nc, ident_bf16[:])
+        one = const.tile([P, 1], F32)
+        nc.vector.memset(one[:], 1.0)
+        warm = const.tile([P, 1], F32)
+        nc.scalar.activation(out=warm[:], in_=one[:], func=FUNC.Sqrt)
+
+        q_raw = [inputs.tile([P, Q_TILES, C], BF16, name="q_raw%d" % b) for b in range(BATCH)]
+        mu_raw = [inputs.tile([P, KEY_TILES, C], BF16, name="mu_raw%d" % b) for b in range(BATCH)]
+        var_raw = [inputs.tile([P, KEY_TILES, C], BF16, name="var_raw%d" % b) for b in range(BATCH)]
+        v_raw = [inputs.tile([P, PACK, C], BF16, name="v_raw%d" % b) for b in range(BATCH)]
+
+        def mx_operand(name, width):
+            codes = keep.tile([P, width], U32, name=name + "_codes", align_bytes=64)
+            scales = keep.tile([P, width], U8, name=name + "_scales", align_bytes=64)
+            return codes, scales
+
+        mu_mx = [mx_operand("mu%d" % b, TK) for b in range(BATCH)]
+        var_mx = [mx_operand("var%d" % b, TK) for b in range(BATCH)]
+        v_mx = [mx_operand("v%d" % b, C) for b in range(BATCH)]
+
+        scores = keep.tile([P, BATCH * Q_TILES, TK], F32)
+        neg_max = keep.tile([P, BATCH * Q_TILES], F32)
+        row_sum = keep.tile([P, BATCH * Q_TILES], F32)
+        inv_sum = keep.tile([P, BATCH * Q_TILES], F32)
+
+        for b in range(BATCH):
+            nc.sync.dma_start(out=mu_raw[b][:], in_=k_mu[b].rearrange("(p t) c -> p t c", t=KEY_TILES))
+            nc.sync.dma_start(out=var_raw[b][:], in_=k_var[b].rearrange("(p t) c -> p t c", t=KEY_TILES))
+            q_rows = q[b].rearrange("(p j) c -> p j c", j=Q_TILES)
+            for j in range(0, Q_TILES, LOAD_TILES):
+                nc.sync.dma_start(out=q_raw[b][:, j : j + LOAD_TILES, :], in_=q_rows[:, j : j + LOAD_TILES, :])
+            nc.sync.dma_start(out=v_raw[b][:], in_=v_sample[b].rearrange("(p t) c -> p t c", t=PACK))
+
+        def turn_pair(rows):
+            turned = psum_turn.tile([P, HALVES, PAIR * P], F32, tag="turned")
+            for r in range(PAIR):
+                words = rows[:, r, :].bitcast(F32)
+                for u in range(HALVES):
+                    nc.tensor.transpose(
+                        turned[:, u, r * P : (r + 1) * P], words[:, u * P : (u + 1) * P], ident_f32[:]
+                    )
+            return turned
+
+        def copy_grouped(turned, grouped):
+            nc.scalar.copy(
+                out=grouped.bitcast(F32).rearrange("p (n u) -> p n u", u=HALVES),
+                in_=turned[:].rearrange("p u n -> p n u"),
+            )
+
+        def prepare_keys(b):
+            for raw, (codes, scales) in ((mu_raw[b], mu_mx[b]), (var_raw[b], var_mx[b])):
+                grouped = kv_stage.tile([P, TK * PACK], BF16, tag="kv_grouped", align_bytes=64)
+                half = PAIR * P * PACK
+                for h in range(KEY_TILES // PAIR):
+                    turned = turn_pair(raw[:, h * PAIR : (h + 1) * PAIR, :])
+                    copy_grouped(turned, grouped[:, h * half : (h + 1) * half])
+                nc.vector.quantize_mx(out=codes[:].bitcast(FP8X4), scales=scales[:], in_=grouped[:])
+
+        def prepare_values(b):
+            codes, scales = v_mx[b]
+            grouped = kv_stage.tile([P, C, PACK], BF16, tag="kv_grouped", align_bytes=64)
+            nc.scalar.copy(out=grouped[:], in_=v_raw[b][:].rearrange("p t c -> p c t"))
+            nc.vector.quantize_mx(
+                out=codes[:].bitcast(FP8X4), scales=scales[:], in_=grouped[:].rearrange("p c t -> p (c t)")
+            )
+
+        q_grouped = {}
+        q_mx = {}
+        mean_ps = {}
+        var_ps = {}
+        penalty = {}
+
+        def turn_queries(s):
+            b, i = divmod(s, PAIRS_PER_BATCH)
+            turned = turn_pair(q_raw[b][:, i * PAIR : (i + 1) * PAIR, :])
+            grouped = q_stage.tile([P, 2, PAIR * P * PACK], BF16, tag="q_grouped", align_bytes=64)
+            copy_grouped(turned, grouped[:, 0, :])
+            q_grouped[s] = grouped
+
+        def square_queries(s):
+            grouped = q_grouped[s]
+            nc.vector.tensor_tensor(out=grouped[:, 1, :], in0=grouped[:, 0, :], in1=grouped[:, 0, :], op=ALU.mult)
+
+        def quantise_queries(s):
+            codes = q_stage.tile([P, 2 * PAIR * P], U32, tag="q_codes", align_bytes=64)
+            scales = q_stage.tile([P, 2 * PAIR * P], U8, tag="q_scales", align_bytes=64)
+            nc.vector.quantize_mx(
+                out=codes[:].bitcast(FP8X4), scales=scales[:], in_=q_grouped[s][:].rearrange("p k n -> p (k n)")
+            )
+            q_mx[s] = (codes, scales)
+
+        def score_passes(s):
+            b = s // PAIRS_PER_BATCH
+            codes, scales = q_mx[s]
+            for r in range(PAIR):
+                for plane, (k_codes, k_scales), banks in ((1, var_mx[b], var_ps), (0, mu_mx[b], mean_ps)):
+                    cols = slice((plane * PAIR + r) * P, (plane * PAIR + r + 1) * P)
+                    bank = psum_acc.tile([P, TK], F32, tag="acc")
+                    nc.tensor.matmul_mx(
+                        out=bank[:],
+                        lhsT=codes[:, cols].bitcast(FP8X4),
+                        lhsT_scale=scales[:, cols],
+                        rhs=k_codes[:].bitcast(FP8X4),
+                        rhs_scale=k_scales[:],
+                        start=True,
+                        stop=True,
+                    )
+                    banks[(s, r)] = bank
+
+        def penalties(s):
+            for r in range(PAIR):
+                pen = pen_stage.tile([P, TK], F32, tag="pen")
+                nc.scalar.activation(out=pen[:], in_=var_ps[(s, r)][:], func=FUNC.Sqrt, scale=BETA * BETA / C)
+                penalty[(s, r)] = pen
+
+        def combine(s, r):
+            nc.vector.scalar_tensor_tensor(
+                out=scores[:, s * PAIR + r, :],
+                in0=mean_ps[(s, r)][:],
+                scalar=1.0 / math.sqrt(C),
+                in1=penalty[(s, r)][:],
+                op0=ALU.mult,
+                op1=ALU.subtract,
+            )
+
+        prepare_keys(0)
+        turn_queries(0)
+        turn_queries(1)
+        turn_queries(2)
+        square_queries(0)
+        square_queries(1)
+        quantise_queries(0)
+        for s in range(N_PAIRS):
+            b, i = divmod(s, PAIRS_PER_BATCH)
+            score_passes(s)
+            penalties(s)
+            if s + 3 < N_PAIRS:
+                turn_queries(s + 3)
+            if s + 1 < N_PAIRS:
+                quantise_queries(s + 1)
+            combine(s, 0)
+            if s + 2 < N_PAIRS:
+                square_queries(s + 2)
+            combine(s, 1)
+            if i == VALUES_AT:
+                prepare_values(b)
+            if i == NEXT_KEYS_AT and b + 1 < BATCH:
+                prepare_keys(b + 1)
+
+        weights = {}
+        w_turned = {}
+        w_grouped = {}
+        w_mx = {}
+        out_ps = {}
+
+        def row_maxima(s):
+            tiles = slice(s * PAIR, (s + 1) * PAIR)
+            nc.vector.tensor_reduce(
+                out=neg_max[:, tiles], in_=scores[:, tiles, :], axis=AXIS.X, op=ALU.max, negate=True
+            )
+
+        def exponentials(s):
+            e = e_stage.tile([P, PAIR, TK], BF16, tag="e")
+            for r in range(PAIR):
+                t = s * PAIR + r
+                nc.scalar.activation(
+                    out=e[:, r, :],
+                    in_=scores[:, t, :],
+                    func=FUNC.Exp,
+                    bias=neg_max[:, t : t + 1],
+                    scale=1.0,
+                    accum_out=row_sum[:, t : t + 1],
+                )
+            weights[s] = e
+
+        def turn_weights(s):
+            turned = psum_turn.tile([P, PAIR, KEY_TILES, P], BF16, tag="turned")
+            for r in range(PAIR):
+                for t in range(KEY_TILES):
+                    nc.tensor.transpose(turned[:, r, t, :], weights[s][:, r, t * P : (t + 1) * P], ident_bf16[:])
+            w_turned[s] = turned
+
+        def group_weights(s):
+            grouped = e_stage.tile([P, PAIR, P, PACK], BF16, tag="w_grouped", align_bytes=64)
+            nc.vector.tensor_copy(out=grouped[:], in_=w_turned[s][:].rearrange("p r t n -> p r n t"))
+            w_grouped[s] = grouped
+
+        def quantise_weights(s):
+            codes = e_stage.tile([P, PAIR * P], U32, tag="w_codes", align_bytes=64)
+            scales = e_stage.tile([P, PAIR * P], U8, tag="w_scales", align_bytes=64)
+            nc.vector.quantize_mx(
+                out=codes[:].bitcast(FP8X4), scales=scales[:], in_=w_grouped[s][:].rearrange("p r n t -> p (r n t)")
+            )
+            w_mx[s] = (codes, scales)
+            tiles = slice(s * PAIR, (s + 1) * PAIR)
+            nc.vector.reciprocal(out=inv_sum[:, tiles], in_=row_sum[:, tiles])
+
+        def out_passes(s):
+            codes, scales = w_mx[s]
+            v_codes, v_scales = v_mx[s // PAIRS_PER_BATCH]
+            for r in range(PAIR):
+                cols = slice(r * P, (r + 1) * P)
+                bank = psum_acc.tile([P, C], F32, tag="acc")
+                nc.tensor.matmul_mx(
+                    out=bank[:],
+                    lhsT=codes[:, cols].bitcast(FP8X4),
+                    lhsT_scale=scales[:, cols],
+                    rhs=v_codes[:].bitcast(FP8X4),
+                    rhs_scale=v_scales[:],
+                    start=True,
+                    stop=True,
+                )
+                out_ps[(s, r)] = bank
+
+        def normalise_and_store(s):
+            b, i = divmod(s, PAIRS_PER_BATCH)
+            result = out_stage.tile([P, PAIR, C], F32, tag="result")
+            for r in range(PAIR):
+                t = s * PAIR + r
+                nc.scalar.activation(
+                    out=result[:, r, :], in_=out_ps[(s, r)][:], func=FUNC.Copy, scale=inv_sum[:, t : t + 1]
+                )
+            out_rows = out[b].rearrange("(p j) c -> p j c", j=Q_TILES)
+            nc.sync.dma_start(out=out_rows[:, i * PAIR : (i + 1) * PAIR, :], in_=result[:])
+
+        row_maxima(0)
+        row_maxima(1)
+        exponentials(0)
+        turn_weights(0)
+        for s in range(N_PAIRS + 1):
+            if s >= 1:
+                out_passes(s - 1)
+            if s + 1 < N_PAIRS:
+                exponentials(s + 1)
+                turn_weights(s + 1)
+            if s >= 1:
+                normalise_and_store(s - 1)
+            if s < N_PAIRS:
+                group_weights(s)
+                if s + 2 < N_PAIRS:
+                    row_maxima(s + 2)
+                quantise_weights(s)

@@ -20,16 +20,19 @@ FLOPS = 3 * 2 * BATCH * TQ * TK * C
 P = 128
 PACK = 4
 HALVES = 2
-WORDS = C // 2
 PAIR = 2
 KEY_TILES = TK // P
 Q_TILES = TQ // P
 PAIRS_PER_BATCH = Q_TILES // PAIR
 N_PAIRS = BATCH * PAIRS_PER_BATCH
-LOAD_TILES = 4
 
-VALUES_AT = 3
-NEXT_KEYS_AT = 5
+NEXT_KEYS_AT = 4
+VALUES_AT = 6
+
+SQUARE_ON_SCALAR = 384
+
+EXP_LEAD = 3
+MAX_LEAD = EXP_LEAD + 1
 
 
 def tile_probcrossattention_pb_t_kernel(tc, q, k_mu, k_var, v_sample, out):
@@ -43,8 +46,9 @@ def tile_probcrossattention_pb_t_kernel(tc, q, k_mu, k_var, v_sample, out):
         kv_stage = ctx.enter_context(tc.tile_pool(name="kv_stage", bufs=2))
         q_stage = ctx.enter_context(tc.tile_pool(name="q_stage", bufs=3))
         pen_stage = ctx.enter_context(tc.tile_pool(name="pen_stage", bufs=4))
+        e_ahead = ctx.enter_context(tc.tile_pool(name="e_ahead", bufs=EXP_LEAD + 2))
         e_stage = ctx.enter_context(tc.tile_pool(name="e_stage", bufs=3))
-        out_stage = ctx.enter_context(tc.tile_pool(name="out_stage", bufs=4))
+        out_stage = ctx.enter_context(tc.tile_pool(name="out_stage", bufs=6))
         psum_turn = ctx.enter_context(tc.psum_pool(name="psum_turn", bufs=2))
         psum_acc = ctx.enter_context(tc.psum_pool(name="psum_acc", bufs=6))
 
@@ -76,12 +80,17 @@ def tile_probcrossattention_pb_t_kernel(tc, q, k_mu, k_var, v_sample, out):
         row_sum = keep.tile([P, BATCH * Q_TILES], F32)
         inv_sum = keep.tile([P, BATCH * Q_TILES], F32)
 
+        def load_queries(s):
+            b, i = divmod(s, PAIRS_PER_BATCH)
+            tiles = slice(i * PAIR, (i + 1) * PAIR)
+            nc.sync.dma_start(out=q_raw[b][:, tiles, :], in_=q[b].rearrange("(p j) c -> p j c", j=Q_TILES)[:, tiles, :])
+
+        load_queries(0)
         for b in range(BATCH):
             nc.sync.dma_start(out=mu_raw[b][:], in_=k_mu[b].rearrange("(p t) c -> p t c", t=KEY_TILES))
             nc.sync.dma_start(out=var_raw[b][:], in_=k_var[b].rearrange("(p t) c -> p t c", t=KEY_TILES))
-            q_rows = q[b].rearrange("(p j) c -> p j c", j=Q_TILES)
-            for j in range(0, Q_TILES, LOAD_TILES):
-                nc.sync.dma_start(out=q_raw[b][:, j : j + LOAD_TILES, :], in_=q_rows[:, j : j + LOAD_TILES, :])
+            for s in range(max(b * PAIRS_PER_BATCH, 1), (b + 1) * PAIRS_PER_BATCH):
+                load_queries(s)
             nc.sync.dma_start(out=v_raw[b][:], in_=v_sample[b].rearrange("(p t) c -> p t c", t=PACK))
 
         def turn_pair(rows):
@@ -94,8 +103,8 @@ def tile_probcrossattention_pb_t_kernel(tc, q, k_mu, k_var, v_sample, out):
                     )
             return turned
 
-        def copy_grouped(turned, grouped):
-            nc.scalar.copy(
+        def copy_grouped(turned, grouped, engine_copy):
+            engine_copy(
                 out=grouped.bitcast(F32).rearrange("p (n u) -> p n u", u=HALVES),
                 in_=turned[:].rearrange("p u n -> p n u"),
             )
@@ -106,13 +115,14 @@ def tile_probcrossattention_pb_t_kernel(tc, q, k_mu, k_var, v_sample, out):
                 half = PAIR * P * PACK
                 for h in range(KEY_TILES // PAIR):
                     turned = turn_pair(raw[:, h * PAIR : (h + 1) * PAIR, :])
-                    copy_grouped(turned, grouped[:, h * half : (h + 1) * half])
+                    engine_copy = nc.scalar.copy if h == 0 else nc.vector.tensor_copy
+                    copy_grouped(turned, grouped[:, h * half : (h + 1) * half], engine_copy)
                 nc.vector.quantize_mx(out=codes[:].bitcast(FP8X4), scales=scales[:], in_=grouped[:])
 
         def prepare_values(b):
             codes, scales = v_mx[b]
             grouped = kv_stage.tile([P, C, PACK], BF16, tag="kv_grouped", align_bytes=64)
-            nc.scalar.copy(out=grouped[:], in_=v_raw[b][:].rearrange("p t c -> p c t"))
+            nc.vector.tensor_copy(out=grouped[:], in_=v_raw[b][:].rearrange("p t c -> p c t"))
             nc.vector.quantize_mx(
                 out=codes[:].bitcast(FP8X4), scales=scales[:], in_=grouped[:].rearrange("p c t -> p (c t)")
             )
@@ -127,12 +137,14 @@ def tile_probcrossattention_pb_t_kernel(tc, q, k_mu, k_var, v_sample, out):
             b, i = divmod(s, PAIRS_PER_BATCH)
             turned = turn_pair(q_raw[b][:, i * PAIR : (i + 1) * PAIR, :])
             grouped = q_stage.tile([P, 2, PAIR * P * PACK], BF16, tag="q_grouped", align_bytes=64)
-            copy_grouped(turned, grouped[:, 0, :])
+            copy_grouped(turned, grouped[:, 0, :], nc.scalar.copy)
             q_grouped[s] = grouped
 
         def square_queries(s):
-            grouped = q_grouped[s]
-            nc.vector.tensor_tensor(out=grouped[:, 1, :], in0=grouped[:, 0, :], in1=grouped[:, 0, :], op=ALU.mult)
+            plain, squared = q_grouped[s][:, 0, :], q_grouped[s][:, 1, :]
+            cut = SQUARE_ON_SCALAR
+            nc.scalar.activation(out=squared[:, :cut], in_=plain[:, :cut], func=FUNC.Square)
+            nc.vector.tensor_tensor(out=squared[:, cut:], in0=plain[:, cut:], in1=plain[:, cut:], op=ALU.mult)
 
         def quantise_queries(s):
             codes = q_stage.tile([P, 2 * PAIR * P], U32, tag="q_codes", align_bytes=64)
@@ -176,13 +188,13 @@ def tile_probcrossattention_pb_t_kernel(tc, q, k_mu, k_var, v_sample, out):
                 op1=ALU.subtract,
             )
 
-        prepare_keys(0)
         turn_queries(0)
+        square_queries(0)
+        prepare_keys(0)
+        quantise_queries(0)
         turn_queries(1)
         turn_queries(2)
-        square_queries(0)
         square_queries(1)
-        quantise_queries(0)
         for s in range(N_PAIRS):
             b, i = divmod(s, PAIRS_PER_BATCH)
             score_passes(s)
@@ -195,10 +207,11 @@ def tile_probcrossattention_pb_t_kernel(tc, q, k_mu, k_var, v_sample, out):
             if s + 2 < N_PAIRS:
                 square_queries(s + 2)
             combine(s, 1)
-            if i == VALUES_AT:
-                prepare_values(b)
             if i == NEXT_KEYS_AT and b + 1 < BATCH:
                 prepare_keys(b + 1)
+            if i == VALUES_AT:
+                prepare_values(b)
+        nc.scalar.activation(out=warm[:], in_=one[:], func=FUNC.Exp)
 
         weights = {}
         w_turned = {}
@@ -213,7 +226,7 @@ def tile_probcrossattention_pb_t_kernel(tc, q, k_mu, k_var, v_sample, out):
             )
 
         def exponentials(s):
-            e = e_stage.tile([P, PAIR, TK], BF16, tag="e")
+            e = e_ahead.tile([P, PAIR, TK], BF16, tag="e")
             for r in range(PAIR):
                 t = s * PAIR + r
                 nc.scalar.activation(
@@ -267,29 +280,36 @@ def tile_probcrossattention_pb_t_kernel(tc, q, k_mu, k_var, v_sample, out):
 
         def normalise_and_store(s):
             b, i = divmod(s, PAIRS_PER_BATCH)
-            result = out_stage.tile([P, PAIR, C], F32, tag="result")
+            out_rows = out[b].rearrange("(p j) c -> p j c", j=Q_TILES)
             for r in range(PAIR):
                 t = s * PAIR + r
-                nc.scalar.activation(
-                    out=result[:, r, :], in_=out_ps[(s, r)][:], func=FUNC.Copy, scale=inv_sum[:, t : t + 1]
-                )
-            out_rows = out[b].rearrange("(p j) c -> p j c", j=Q_TILES)
-            nc.sync.dma_start(out=out_rows[:, i * PAIR : (i + 1) * PAIR, :], in_=result[:])
+                result = out_stage.tile([P, C], F32, tag="result")
+                if s == N_PAIRS - 1 and r == PAIR - 1:
+                    nc.vector.tensor_scalar(
+                        out=result[:], in0=out_ps[(s, r)][:], scalar1=inv_sum[:, t : t + 1], scalar2=None, op0=ALU.mult
+                    )
+                else:
+                    nc.scalar.activation(
+                        out=result[:], in_=out_ps[(s, r)][:], func=FUNC.Copy, scale=inv_sum[:, t : t + 1]
+                    )
+                nc.sync.dma_start(out=out_rows[:, i * PAIR + r, :], in_=result[:])
 
-        row_maxima(0)
-        row_maxima(1)
-        exponentials(0)
+        for s in range(MAX_LEAD):
+            row_maxima(s)
+        for s in range(EXP_LEAD):
+            exponentials(s)
         turn_weights(0)
         for s in range(N_PAIRS + 1):
             if s >= 1:
                 out_passes(s - 1)
+            if s + EXP_LEAD < N_PAIRS:
+                exponentials(s + EXP_LEAD)
             if s + 1 < N_PAIRS:
-                exponentials(s + 1)
                 turn_weights(s + 1)
             if s >= 1:
                 normalise_and_store(s - 1)
             if s < N_PAIRS:
                 group_weights(s)
-                if s + 2 < N_PAIRS:
-                    row_maxima(s + 2)
+                if s + MAX_LEAD < N_PAIRS:
+                    row_maxima(s + MAX_LEAD)
                 quantise_weights(s)

@@ -25,14 +25,24 @@ KEY_TILES = TK // P
 Q_TILES = TQ // P
 PAIRS_PER_BATCH = Q_TILES // PAIR
 N_PAIRS = BATCH * PAIRS_PER_BATCH
+PSUM_BANKS = 8
 
-NEXT_KEYS_AT = 4
-VALUES_AT = 6
+SQUARE_LEAD = 1
+GROUP_LEAD = 2
+TURN_LEAD = 4
+SQRT_LEAD = 1
+SCORE_LEAD = 2
+MAX_LEAD = 4
+EXP_LEAD = 3
+TURN_E_LEAD = 1
+OUT_LAG = 1
+STORE_LAG = 2
 
 SQUARE_ON_SCALAR = 384
 
-EXP_LEAD = 3
-MAX_LEAD = EXP_LEAD + 1
+
+def live(s):
+    return 0 <= s < N_PAIRS
 
 
 def tile_probcrossattention_pb_t_kernel(tc, q, k_mu, k_var, v_sample, out):
@@ -41,16 +51,9 @@ def tile_probcrossattention_pb_t_kernel(tc, q, k_mu, k_var, v_sample, out):
         ctx.enter_context(tc.manual_schedule())
 
         const = ctx.enter_context(tc.tile_pool(name="const", bufs=1))
-        inputs = ctx.enter_context(tc.tile_pool(name="inputs", bufs=1))
         keep = ctx.enter_context(tc.tile_pool(name="keep", bufs=1))
-        kv_stage = ctx.enter_context(tc.tile_pool(name="kv_stage", bufs=2))
-        q_stage = ctx.enter_context(tc.tile_pool(name="q_stage", bufs=3))
-        pen_stage = ctx.enter_context(tc.tile_pool(name="pen_stage", bufs=4))
-        e_ahead = ctx.enter_context(tc.tile_pool(name="e_ahead", bufs=EXP_LEAD + 2))
-        e_stage = ctx.enter_context(tc.tile_pool(name="e_stage", bufs=3))
-        out_stage = ctx.enter_context(tc.tile_pool(name="out_stage", bufs=6))
-        psum_turn = ctx.enter_context(tc.psum_pool(name="psum_turn", bufs=2))
-        psum_acc = ctx.enter_context(tc.psum_pool(name="psum_acc", bufs=6))
+        psum = ctx.enter_context(tc.psum_pool(name="psum", bufs=PSUM_BANKS))
+        pen_stage = ctx.enter_context(tc.tile_pool(name="pen_stage", bufs=3 * PAIR))
 
         ident_f32 = const.tile([P, P], F32)
         make_identity(nc, ident_f32[:])
@@ -61,255 +64,222 @@ def tile_probcrossattention_pb_t_kernel(tc, q, k_mu, k_var, v_sample, out):
         warm = const.tile([P, 1], F32)
         nc.scalar.activation(out=warm[:], in_=one[:], func=FUNC.Sqrt)
 
-        q_raw = [inputs.tile([P, Q_TILES, C], BF16, name="q_raw%d" % b) for b in range(BATCH)]
-        mu_raw = [inputs.tile([P, KEY_TILES, C], BF16, name="mu_raw%d" % b) for b in range(BATCH)]
-        var_raw = [inputs.tile([P, KEY_TILES, C], BF16, name="var_raw%d" % b) for b in range(BATCH)]
-        v_raw = [inputs.tile([P, PACK, C], BF16, name="v_raw%d" % b) for b in range(BATCH)]
-
         def mx_operand(name, width):
             codes = keep.tile([P, width], U32, name=name + "_codes", align_bytes=64)
             scales = keep.tile([P, width], U8, name=name + "_scales", align_bytes=64)
             return codes, scales
 
-        mu_mx = [mx_operand("mu%d" % b, TK) for b in range(BATCH)]
         var_mx = [mx_operand("var%d" % b, TK) for b in range(BATCH)]
+        mu_mx = [mx_operand("mu%d" % b, TK) for b in range(BATCH)]
         v_mx = [mx_operand("v%d" % b, C) for b in range(BATCH)]
+        q_mx = [mx_operand("q%d" % s, 2 * PAIR * P) for s in range(N_PAIRS)]
 
-        scores = keep.tile([P, BATCH * Q_TILES, TK], F32)
-        neg_max = keep.tile([P, BATCH * Q_TILES], F32)
-        row_sum = keep.tile([P, BATCH * Q_TILES], F32)
-        inv_sum = keep.tile([P, BATCH * Q_TILES], F32)
+        scores = keep.tile([P, N_PAIRS * PAIR, TK], F32)
+        neg_max = keep.tile([P, N_PAIRS * PAIR], F32)
+        row_sum = keep.tile([P, N_PAIRS * PAIR], F32)
+        inv_sum = keep.tile([P, N_PAIRS * PAIR], F32)
 
-        def load_queries(s):
-            b, i = divmod(s, PAIRS_PER_BATCH)
-            tiles = slice(i * PAIR, (i + 1) * PAIR)
-            nc.sync.dma_start(out=q_raw[b][:, tiles, :], in_=q[b].rearrange("(p j) c -> p j c", j=Q_TILES)[:, tiles, :])
+        with ExitStack() as phase0:
+            inputs = phase0.enter_context(tc.tile_pool(name="inputs", bufs=1))
+            k_stage = phase0.enter_context(tc.tile_pool(name="k_stage", bufs=2))
+            v_stage = phase0.enter_context(tc.tile_pool(name="v_stage", bufs=1))
+            q_stage = phase0.enter_context(tc.tile_pool(name="q_stage", bufs=GROUP_LEAD + 2))
 
-        load_queries(0)
-        for b in range(BATCH):
-            nc.sync.dma_start(out=mu_raw[b][:], in_=k_mu[b].rearrange("(p t) c -> p t c", t=KEY_TILES))
-            nc.sync.dma_start(out=var_raw[b][:], in_=k_var[b].rearrange("(p t) c -> p t c", t=KEY_TILES))
-            for s in range(max(b * PAIRS_PER_BATCH, 1), (b + 1) * PAIRS_PER_BATCH):
-                load_queries(s)
-            nc.sync.dma_start(out=v_raw[b][:], in_=v_sample[b].rearrange("(p t) c -> p t c", t=PACK))
+            q_raw = [inputs.tile([P, Q_TILES, C], BF16, name="q_raw%d" % b) for b in range(BATCH)]
+            var_raw = [inputs.tile([P, KEY_TILES, C], BF16, name="var_raw%d" % b) for b in range(BATCH)]
+            mu_raw = [inputs.tile([P, KEY_TILES, C], BF16, name="mu_raw%d" % b) for b in range(BATCH)]
+            v_raw = [inputs.tile([P, PACK, C], BF16, name="v_raw%d" % b) for b in range(BATCH)]
 
-        def turn_pair(rows):
-            turned = psum_turn.tile([P, HALVES, PAIR * P], F32, tag="turned")
-            for r in range(PAIR):
-                words = rows[:, r, :].bitcast(F32)
-                for u in range(HALVES):
-                    nc.tensor.transpose(
-                        turned[:, u, r * P : (r + 1) * P], words[:, u * P : (u + 1) * P], ident_f32[:]
+            def load_queries(b):
+                for i in range(PAIRS_PER_BATCH):
+                    tiles = slice(i * PAIR, (i + 1) * PAIR)
+                    nc.sync.dma_start(
+                        out=q_raw[b][:, tiles, :], in_=q[b].rearrange("(p j) c -> p j c", j=Q_TILES)[:, tiles, :]
                     )
-            return turned
 
-        def copy_grouped(turned, grouped, engine_copy):
-            engine_copy(
-                out=grouped.bitcast(F32).rearrange("p (n u) -> p n u", u=HALVES),
-                in_=turned[:].rearrange("p u n -> p n u"),
-            )
+            load_queries(0)
+            for b in range(BATCH):
+                nc.sync.dma_start(out=v_raw[b][:], in_=v_sample[b].rearrange("(p t) c -> p t c", t=PACK))
+                nc.sync.dma_start(out=var_raw[b][:], in_=k_var[b].rearrange("(p t) c -> p t c", t=KEY_TILES))
+                nc.sync.dma_start(out=mu_raw[b][:], in_=k_mu[b].rearrange("(p t) c -> p t c", t=KEY_TILES))
+            load_queries(1)
 
-        def prepare_keys(b):
-            for raw, (codes, scales) in ((mu_raw[b], mu_mx[b]), (var_raw[b], var_mx[b])):
-                grouped = kv_stage.tile([P, TK * PACK], BF16, tag="kv_grouped", align_bytes=64)
-                half = PAIR * P * PACK
-                for h in range(KEY_TILES // PAIR):
-                    turned = turn_pair(raw[:, h * PAIR : (h + 1) * PAIR, :])
-                    engine_copy = nc.scalar.copy if h == 0 else nc.vector.tensor_copy
-                    copy_grouped(turned, grouped[:, h * half : (h + 1) * half], engine_copy)
-                nc.vector.quantize_mx(out=codes[:].bitcast(FP8X4), scales=scales[:], in_=grouped[:])
+            def turn_pair(rows):
+                turned = psum.tile([P, HALVES, PAIR * P], F32, tag="bank")
+                for r in range(PAIR):
+                    words = rows[:, r, :].bitcast(F32)
+                    for u in range(HALVES):
+                        nc.tensor.transpose(
+                            turned[:, u, r * P : (r + 1) * P], words[:, u * P : (u + 1) * P], ident_f32[:]
+                        )
+                return turned
 
-        def prepare_values(b):
-            codes, scales = v_mx[b]
-            grouped = kv_stage.tile([P, C, PACK], BF16, tag="kv_grouped", align_bytes=64)
-            nc.vector.tensor_copy(out=grouped[:], in_=v_raw[b][:].rearrange("p t c -> p c t"))
-            nc.vector.quantize_mx(
-                out=codes[:].bitcast(FP8X4), scales=scales[:], in_=grouped[:].rearrange("p c t -> p (c t)")
-            )
+            def copy_grouped(turned, grouped):
+                nc.scalar.copy(
+                    out=grouped.bitcast(F32).rearrange("p (n u) -> p n u", u=HALVES),
+                    in_=turned[:].rearrange("p u n -> p n u"),
+                )
 
-        q_grouped = {}
-        q_mx = {}
-        mean_ps = {}
+            def prepare_keys_and_values(b):
+                v_grouped = v_stage.tile([P, C, PACK], BF16, align_bytes=64)
+                nc.vector.tensor_copy(out=v_grouped[:], in_=v_raw[b][:].rearrange("p t c -> p c t"))
+                for raw, (codes, scales) in ((var_raw[b], var_mx[b]), (mu_raw[b], mu_mx[b])):
+                    k_grouped = k_stage.tile([P, TK * PACK], BF16, align_bytes=64)
+                    half = PAIR * P * PACK
+                    for h in range(KEY_TILES // PAIR):
+                        turned = turn_pair(raw[:, h * PAIR : (h + 1) * PAIR, :])
+                        copy_grouped(turned, k_grouped[:, h * half : (h + 1) * half])
+                    nc.vector.quantize_mx(out=codes[:].bitcast(FP8X4), scales=scales[:], in_=k_grouped[:])
+                codes, scales = v_mx[b]
+                nc.vector.quantize_mx(
+                    out=codes[:].bitcast(FP8X4), scales=scales[:], in_=v_grouped[:].rearrange("p c t -> p (c t)")
+                )
+
+            def prepare_queries(b):
+                q_turned = {}
+                q_grouped = {}
+                for step in range(-TURN_LEAD, PAIRS_PER_BATCH):
+                    i = step + TURN_LEAD
+                    if i < PAIRS_PER_BATCH:
+                        q_turned[i] = turn_pair(q_raw[b][:, i * PAIR : (i + 1) * PAIR, :])
+                    i = step + GROUP_LEAD
+                    if 0 <= i < PAIRS_PER_BATCH:
+                        q_grouped[i] = q_stage.tile([P, 2, PAIR * P * PACK], BF16, name="q_grouped", align_bytes=64)
+                        copy_grouped(q_turned[i], q_grouped[i][:, 0, :])
+                    i = step + SQUARE_LEAD
+                    if 0 <= i < PAIRS_PER_BATCH:
+                        plain, squared = q_grouped[i][:, 0, :], q_grouped[i][:, 1, :]
+                        cut = SQUARE_ON_SCALAR
+                        nc.scalar.activation(out=squared[:, :cut], in_=plain[:, :cut], func=FUNC.Square)
+                        nc.vector.tensor_tensor(
+                            out=squared[:, cut:], in0=plain[:, cut:], in1=plain[:, cut:], op=ALU.mult
+                        )
+                    i = step
+                    if 0 <= i:
+                        codes, scales = q_mx[b * PAIRS_PER_BATCH + i]
+                        nc.vector.quantize_mx(
+                            out=codes[:].bitcast(FP8X4), scales=scales[:], in_=q_grouped[i][:].rearrange("p k n -> p (k n)")
+                        )
+
+            prepare_queries(0)
+            prepare_keys_and_values(0)
+            prepare_keys_and_values(1)
+            prepare_queries(1)
+
         var_ps = {}
+        mean_ps = {}
         penalty = {}
-
-        def turn_queries(s):
-            b, i = divmod(s, PAIRS_PER_BATCH)
-            turned = turn_pair(q_raw[b][:, i * PAIR : (i + 1) * PAIR, :])
-            grouped = q_stage.tile([P, 2, PAIR * P * PACK], BF16, tag="q_grouped", align_bytes=64)
-            copy_grouped(turned, grouped[:, 0, :], nc.scalar.copy)
-            q_grouped[s] = grouped
-
-        def square_queries(s):
-            plain, squared = q_grouped[s][:, 0, :], q_grouped[s][:, 1, :]
-            cut = SQUARE_ON_SCALAR
-            nc.scalar.activation(out=squared[:, :cut], in_=plain[:, :cut], func=FUNC.Square)
-            nc.vector.tensor_tensor(out=squared[:, cut:], in0=plain[:, cut:], in1=plain[:, cut:], op=ALU.mult)
-
-        def quantise_queries(s):
-            codes = q_stage.tile([P, 2 * PAIR * P], U32, tag="q_codes", align_bytes=64)
-            scales = q_stage.tile([P, 2 * PAIR * P], U8, tag="q_scales", align_bytes=64)
-            nc.vector.quantize_mx(
-                out=codes[:].bitcast(FP8X4), scales=scales[:], in_=q_grouped[s][:].rearrange("p k n -> p (k n)")
-            )
-            q_mx[s] = (codes, scales)
-
-        def score_passes(s):
-            b = s // PAIRS_PER_BATCH
-            codes, scales = q_mx[s]
-            for r in range(PAIR):
-                for plane, (k_codes, k_scales), banks in ((1, var_mx[b], var_ps), (0, mu_mx[b], mean_ps)):
-                    cols = slice((plane * PAIR + r) * P, (plane * PAIR + r + 1) * P)
-                    bank = psum_acc.tile([P, TK], F32, tag="acc")
-                    nc.tensor.matmul_mx(
-                        out=bank[:],
-                        lhsT=codes[:, cols].bitcast(FP8X4),
-                        lhsT_scale=scales[:, cols],
-                        rhs=k_codes[:].bitcast(FP8X4),
-                        rhs_scale=k_scales[:],
-                        start=True,
-                        stop=True,
+        for step in range(-SCORE_LEAD, N_PAIRS):
+            s = step
+            if live(s):
+                for r in range(PAIR):
+                    nc.vector.scalar_tensor_tensor(
+                        out=scores[:, s * PAIR + r, :],
+                        in0=mean_ps[(s, r)][:],
+                        scalar=1.0 / math.sqrt(C),
+                        in1=penalty[(s, r)][:],
+                        op0=ALU.mult,
+                        op1=ALU.subtract,
                     )
-                    banks[(s, r)] = bank
-
-        def penalties(s):
-            for r in range(PAIR):
-                pen = pen_stage.tile([P, TK], F32, tag="pen")
-                nc.scalar.activation(out=pen[:], in_=var_ps[(s, r)][:], func=FUNC.Sqrt, scale=BETA * BETA / C)
-                penalty[(s, r)] = pen
-
-        def combine(s, r):
-            nc.vector.scalar_tensor_tensor(
-                out=scores[:, s * PAIR + r, :],
-                in0=mean_ps[(s, r)][:],
-                scalar=1.0 / math.sqrt(C),
-                in1=penalty[(s, r)][:],
-                op0=ALU.mult,
-                op1=ALU.subtract,
-            )
-
-        turn_queries(0)
-        square_queries(0)
-        prepare_keys(0)
-        quantise_queries(0)
-        turn_queries(1)
-        turn_queries(2)
-        square_queries(1)
-        for s in range(N_PAIRS):
-            b, i = divmod(s, PAIRS_PER_BATCH)
-            score_passes(s)
-            penalties(s)
-            if s + 3 < N_PAIRS:
-                turn_queries(s + 3)
-            if s + 1 < N_PAIRS:
-                quantise_queries(s + 1)
-            combine(s, 0)
-            if s + 2 < N_PAIRS:
-                square_queries(s + 2)
-            combine(s, 1)
-            if i == NEXT_KEYS_AT and b + 1 < BATCH:
-                prepare_keys(b + 1)
-            if i == VALUES_AT:
-                prepare_values(b)
-        nc.scalar.activation(out=warm[:], in_=one[:], func=FUNC.Exp)
-
-        weights = {}
-        w_turned = {}
-        w_grouped = {}
-        w_mx = {}
-        out_ps = {}
-
-        def row_maxima(s):
-            tiles = slice(s * PAIR, (s + 1) * PAIR)
-            nc.vector.tensor_reduce(
-                out=neg_max[:, tiles], in_=scores[:, tiles, :], axis=AXIS.X, op=ALU.max, negate=True
-            )
-
-        def exponentials(s):
-            e = e_ahead.tile([P, PAIR, TK], BF16, tag="e")
-            for r in range(PAIR):
-                t = s * PAIR + r
-                nc.scalar.activation(
-                    out=e[:, r, :],
-                    in_=scores[:, t, :],
-                    func=FUNC.Exp,
-                    bias=neg_max[:, t : t + 1],
-                    scale=1.0,
-                    accum_out=row_sum[:, t : t + 1],
-                )
-            weights[s] = e
-
-        def turn_weights(s):
-            turned = psum_turn.tile([P, PAIR, KEY_TILES, P], BF16, tag="turned")
-            for r in range(PAIR):
-                for t in range(KEY_TILES):
-                    nc.tensor.transpose(turned[:, r, t, :], weights[s][:, r, t * P : (t + 1) * P], ident_bf16[:])
-            w_turned[s] = turned
-
-        def group_weights(s):
-            grouped = e_stage.tile([P, PAIR, P, PACK], BF16, tag="w_grouped", align_bytes=64)
-            nc.vector.tensor_copy(out=grouped[:], in_=w_turned[s][:].rearrange("p r t n -> p r n t"))
-            w_grouped[s] = grouped
-
-        def quantise_weights(s):
-            codes = e_stage.tile([P, PAIR * P], U32, tag="w_codes", align_bytes=64)
-            scales = e_stage.tile([P, PAIR * P], U8, tag="w_scales", align_bytes=64)
-            nc.vector.quantize_mx(
-                out=codes[:].bitcast(FP8X4), scales=scales[:], in_=w_grouped[s][:].rearrange("p r n t -> p (r n t)")
-            )
-            w_mx[s] = (codes, scales)
-            tiles = slice(s * PAIR, (s + 1) * PAIR)
-            nc.vector.reciprocal(out=inv_sum[:, tiles], in_=row_sum[:, tiles])
-
-        def out_passes(s):
-            codes, scales = w_mx[s]
-            v_codes, v_scales = v_mx[s // PAIRS_PER_BATCH]
-            for r in range(PAIR):
-                cols = slice(r * P, (r + 1) * P)
-                bank = psum_acc.tile([P, C], F32, tag="acc")
-                nc.tensor.matmul_mx(
-                    out=bank[:],
-                    lhsT=codes[:, cols].bitcast(FP8X4),
-                    lhsT_scale=scales[:, cols],
-                    rhs=v_codes[:].bitcast(FP8X4),
-                    rhs_scale=v_scales[:],
-                    start=True,
-                    stop=True,
-                )
-                out_ps[(s, r)] = bank
-
-        def normalise_and_store(s):
-            b, i = divmod(s, PAIRS_PER_BATCH)
-            out_rows = out[b].rearrange("(p j) c -> p j c", j=Q_TILES)
-            for r in range(PAIR):
-                t = s * PAIR + r
-                result = out_stage.tile([P, C], F32, tag="result")
-                if s == N_PAIRS - 1 and r == PAIR - 1:
-                    nc.vector.tensor_scalar(
-                        out=result[:], in0=out_ps[(s, r)][:], scalar1=inv_sum[:, t : t + 1], scalar2=None, op0=ALU.mult
-                    )
-                else:
+            s = step + SQRT_LEAD
+            if live(s):
+                for r in range(PAIR):
+                    penalty[(s, r)] = pen_stage.tile([P, TK], F32, name="penalty")
                     nc.scalar.activation(
-                        out=result[:], in_=out_ps[(s, r)][:], func=FUNC.Copy, scale=inv_sum[:, t : t + 1]
+                        out=penalty[(s, r)][:], in_=var_ps[(s, r)][:], func=FUNC.Sqrt, scale=BETA * BETA / C
                     )
-                nc.sync.dma_start(out=out_rows[:, i * PAIR + r, :], in_=result[:])
+            s = step + SCORE_LEAD
+            if live(s):
+                b = s // PAIRS_PER_BATCH
+                codes, scales = q_mx[s]
+                for plane, (k_codes, k_scales), banks in ((1, var_mx[b], var_ps), (0, mu_mx[b], mean_ps)):
+                    for r in range(PAIR):
+                        cols = slice((plane * PAIR + r) * P, (plane * PAIR + r + 1) * P)
+                        banks[(s, r)] = psum.tile([P, TK], F32, name="product", tag="bank")
+                        nc.tensor.matmul_mx(
+                            out=banks[(s, r)][:],
+                            lhsT=codes[:, cols].bitcast(FP8X4),
+                            lhsT_scale=scales[:, cols],
+                            rhs=k_codes[:].bitcast(FP8X4),
+                            rhs_scale=k_scales[:],
+                            start=True,
+                            stop=True,
+                        )
 
-        for s in range(MAX_LEAD):
-            row_maxima(s)
-        for s in range(EXP_LEAD):
-            exponentials(s)
-        turn_weights(0)
-        for s in range(N_PAIRS + 1):
-            if s >= 1:
-                out_passes(s - 1)
-            if s + EXP_LEAD < N_PAIRS:
-                exponentials(s + EXP_LEAD)
-            if s + 1 < N_PAIRS:
-                turn_weights(s + 1)
-            if s >= 1:
-                normalise_and_store(s - 1)
-            if s < N_PAIRS:
-                group_weights(s)
-                if s + MAX_LEAD < N_PAIRS:
-                    row_maxima(s + MAX_LEAD)
-                quantise_weights(s)
+        with ExitStack() as phase2:
+            e_ahead = phase2.enter_context(tc.tile_pool(name="e_ahead", bufs=EXP_LEAD + 2))
+            e_stage = phase2.enter_context(tc.tile_pool(name="e_stage", bufs=3))
+            out_stage = phase2.enter_context(tc.tile_pool(name="out_stage", bufs=8))
+            nc.scalar.activation(out=warm[:], in_=one[:], func=FUNC.Exp)
+
+            e = {}
+            e_turned = {}
+            e_mx = {}
+            out_ps = {}
+            for step in range(-MAX_LEAD, N_PAIRS + STORE_LAG):
+                s = step + TURN_E_LEAD
+                if live(s):
+                    e_turned[s] = psum.tile([P, PAIR, KEY_TILES, P], BF16, name="e_turned", tag="bank")
+                    for r in range(PAIR):
+                        for t in range(KEY_TILES):
+                            nc.tensor.transpose(e_turned[s][:, r, t, :], e[s][:, r, t * P : (t + 1) * P], ident_bf16[:])
+                s = step - OUT_LAG
+                if live(s):
+                    codes, scales = e_mx[s]
+                    v_codes, v_scales = v_mx[s // PAIRS_PER_BATCH]
+                    for r in range(PAIR):
+                        cols = slice(r * P, (r + 1) * P)
+                        out_ps[(s, r)] = psum.tile([P, C], F32, name="out_ps", tag="bank")
+                        nc.tensor.matmul_mx(
+                            out=out_ps[(s, r)][:],
+                            lhsT=codes[:, cols].bitcast(FP8X4),
+                            lhsT_scale=scales[:, cols],
+                            rhs=v_codes[:].bitcast(FP8X4),
+                            rhs_scale=v_scales[:],
+                            start=True,
+                            stop=True,
+                        )
+                s = step + EXP_LEAD
+                if live(s):
+                    e[s] = e_ahead.tile([P, PAIR, TK], BF16, name="e")
+                    for r in range(PAIR):
+                        t = s * PAIR + r
+                        nc.scalar.activation(
+                            out=e[s][:, r, :],
+                            in_=scores[:, t, :],
+                            func=FUNC.Exp,
+                            bias=neg_max[:, t : t + 1],
+                            scale=1.0,
+                            accum_out=row_sum[:, t : t + 1],
+                        )
+                s = step - STORE_LAG
+                if live(s):
+                    b, i = divmod(s, PAIRS_PER_BATCH)
+                    out_rows = out[b].rearrange("(p j) c -> p j c", j=Q_TILES)
+                    for r in range(PAIR):
+                        t = s * PAIR + r
+                        result = out_stage.tile([P, C], F32)
+                        nc.scalar.activation(
+                            out=result[:], in_=out_ps[(s, r)][:], func=FUNC.Copy, scale=inv_sum[:, t : t + 1]
+                        )
+                        nc.sync.dma_start(out=out_rows[:, i * PAIR + r, :], in_=result[:])
+                s = step
+                if live(s):
+                    e_grouped = e_stage.tile([P, PAIR, P, PACK], BF16, align_bytes=64)
+                    nc.vector.tensor_copy(out=e_grouped[:], in_=e_turned[s][:].rearrange("p r t n -> p r n t"))
+                s = step + MAX_LEAD
+                if live(s):
+                    tiles = slice(s * PAIR, (s + 1) * PAIR)
+                    nc.vector.tensor_reduce(
+                        out=neg_max[:, tiles], in_=scores[:, tiles, :], axis=AXIS.X, op=ALU.max, negate=True
+                    )
+                s = step
+                if live(s):
+                    codes = e_stage.tile([P, PAIR * P], U32, name="e_codes", align_bytes=64)
+                    scales = e_stage.tile([P, PAIR * P], U8, name="e_scales", align_bytes=64)
+                    nc.vector.quantize_mx(
+                        out=codes[:].bitcast(FP8X4), scales=scales[:], in_=e_grouped[:].rearrange("p r n t -> p (r n t)")
+                    )
+                    e_mx[s] = (codes, scales)
+                    tiles = slice(s * PAIR, (s + 1) * PAIR)
+                    nc.vector.reciprocal(out=inv_sum[:, tiles], in_=row_sum[:, tiles])

@@ -57,8 +57,6 @@ def tile_probcrossattention_pb_t_kernel(tc, q, k_mu, k_var, v_sample, out):
 
         ident_f32 = const.tile([P, P], F32)
         make_identity(nc, ident_f32[:])
-        ident_bf16 = const.tile([P, P], BF16)
-        make_identity(nc, ident_bf16[:])
         one = const.tile([P, 1], F32)
         nc.vector.memset(one[:], 1.0)
         warm = const.tile([P, 1], F32)
@@ -120,6 +118,12 @@ def tile_probcrossattention_pb_t_kernel(tc, q, k_mu, k_var, v_sample, out):
                     in_=turned[:].rearrange("p u n -> p n u"),
                 )
 
+            def copy_keys_grouped(turned, grouped):
+                nc.scalar.copy(
+                    out=grouped.bitcast(F32).rearrange("p (n r u) -> p n r u", r=PAIR, u=HALVES),
+                    in_=turned[:].rearrange("p u (r n) -> p n r u", r=PAIR),
+                )
+
             def prepare_keys_and_values(b):
                 v_grouped = v_stage.tile([P, C, PACK], BF16, align_bytes=64)
                 nc.vector.tensor_copy(out=v_grouped[:], in_=v_raw[b][:].rearrange("p t c -> p c t"))
@@ -128,7 +132,7 @@ def tile_probcrossattention_pb_t_kernel(tc, q, k_mu, k_var, v_sample, out):
                     half = PAIR * P * PACK
                     for h in range(KEY_TILES // PAIR):
                         turned = turn_pair(raw[:, h * PAIR : (h + 1) * PAIR, :])
-                        copy_grouped(turned, k_grouped[:, h * half : (h + 1) * half])
+                        copy_keys_grouped(turned, k_grouped[:, h * half : (h + 1) * half])
                     nc.vector.quantize_mx(out=codes[:].bitcast(FP8X4), scales=scales[:], in_=k_grouped[:])
                 codes, scales = v_mx[b]
                 nc.vector.quantize_mx(
@@ -219,10 +223,11 @@ def tile_probcrossattention_pb_t_kernel(tc, q, k_mu, k_var, v_sample, out):
             for step in range(-MAX_LEAD, N_PAIRS + STORE_LAG):
                 s = step + TURN_E_LEAD
                 if live(s):
-                    e_turned[s] = psum.tile([P, PAIR, KEY_TILES, P], BF16, name="e_turned", tag="bank")
+                    e_turned[s] = psum.tile([P, PAIR, HALVES, P], F32, name="e_turned", tag="bank")
                     for r in range(PAIR):
-                        for t in range(KEY_TILES):
-                            nc.tensor.transpose(e_turned[s][:, r, t, :], e[s][:, r, t * P : (t + 1) * P], ident_bf16[:])
+                        words = e[s][:, r, :].bitcast(F32)
+                        for u in range(HALVES):
+                            nc.tensor.transpose(e_turned[s][:, r, u, :], words[:, u * P : (u + 1) * P], ident_f32[:])
                 s = step - OUT_LAG
                 if live(s):
                     codes, scales = e_mx[s]
@@ -266,7 +271,12 @@ def tile_probcrossattention_pb_t_kernel(tc, q, k_mu, k_var, v_sample, out):
                 s = step
                 if live(s):
                     e_grouped = e_stage.tile([P, PAIR, P, PACK], BF16, align_bytes=64)
-                    nc.vector.tensor_copy(out=e_grouped[:], in_=e_turned[s][:].rearrange("p r t n -> p r n t"))
+                    nc.vector.tensor_copy(
+                        out=e_grouped[:].rearrange("p r n t -> p (r n t)").bitcast(F32).rearrange(
+                            "p (r n u) -> p r n u", r=PAIR, u=HALVES
+                        ),
+                        in_=e_turned[s][:].rearrange("p r u n -> p r n u"),
+                    )
                 s = step + MAX_LEAD
                 if live(s):
                     tiles = slice(s * PAIR, (s + 1) * PAIR)

@@ -40,6 +40,8 @@ STORE_LAG = 2
 
 SQUARE_ON_SCALAR = 384
 
+DIVIDE_ON_VECTOR_EVERY = 3
+
 
 def live(s):
     return 0 <= s < N_PAIRS
@@ -60,6 +62,8 @@ def tile_probcrossattention_pb_t_kernel(tc, q, k_mu, k_var, v_sample, out):
         one = const.tile([P, 1], F32)
         nc.vector.memset(one[:], 1.0)
         warm = const.tile([P, 1], F32)
+        minus_one = const.tile([P, PAIR], F32)
+        nc.vector.memset(minus_one[:], -1.0)
         nc.scalar.activation(out=warm[:], in_=one[:], func=FUNC.Sqrt)
 
         def mx_operand(name, width):
@@ -264,9 +268,12 @@ def tile_probcrossattention_pb_t_kernel(tc, q, k_mu, k_var, v_sample, out):
                     for r in range(PAIR):
                         t = s * PAIR + r
                         result = out_stage.tile([P, C], F32)
-                        nc.scalar.activation(
-                            out=result[:], in_=out_ps[(s, r)][:], func=FUNC.Copy, scale=inv_sum[:, t : t + 1]
-                        )
+                        if r == 1 and s % DIVIDE_ON_VECTOR_EVERY == 0:
+                            nc.vector.tensor_scalar_mul(out=result[:], in0=out_ps[(s, r)][:], scalar1=inv_sum[:, t : t + 1])
+                        else:
+                            nc.scalar.activation(
+                                out=result[:], in_=out_ps[(s, r)][:], func=FUNC.Copy, scale=inv_sum[:, t : t + 1]
+                            )
                         nc.sync.dma_start(out=out_rows[:, i * PAIR + r, :], in_=result[:])
                 s = step
                 if live(s):
@@ -292,4 +299,4 @@ def tile_probcrossattention_pb_t_kernel(tc, q, k_mu, k_var, v_sample, out):
                     )
                     e_mx[s] = (codes, scales)
                     tiles = slice(s * PAIR, (s + 1) * PAIR)
-                    nc.vector.reciprocal(out=inv_sum[:, tiles], in_=row_sum[:, tiles])
+                    nc.gpsimd.tensor_tensor(out=inv_sum[:, tiles], in0=row_sum[:, tiles], in1=minus_one[:], op=ALU.pow)

@@ -32,15 +32,15 @@ GROUP_LEAD = 2
 TURN_LEAD = 4
 SQRT_LEAD = 1
 SCORE_LEAD = 2
-MAX_LEAD = 4
+MAX_LEAD = 5
 EXP_LEAD = 3
 TURN_E_LEAD = 1
 OUT_LAG = 1
 STORE_LAG = 2
 
-SQUARE_ON_SCALAR = 384
+SQUARE_ON_SCALAR = 256
 
-DIVIDE_ON_VECTOR_EVERY = 3
+DIVIDE_ON_VECTOR_EVERY = 4
 
 
 def live(s):
@@ -84,13 +84,11 @@ def tile_probcrossattention_pb_t_kernel(tc, q, k_mu, k_var, v_sample, out):
         with ExitStack() as phase0:
             inputs = phase0.enter_context(tc.tile_pool(name="inputs", bufs=1))
             k_stage = phase0.enter_context(tc.tile_pool(name="k_stage", bufs=2))
-            v_stage = phase0.enter_context(tc.tile_pool(name="v_stage", bufs=1))
             q_stage = phase0.enter_context(tc.tile_pool(name="q_stage", bufs=GROUP_LEAD + 2))
 
-            q_raw = [inputs.tile([P, Q_TILES, C], BF16, name="q_raw%d" % b) for b in range(BATCH)]
+            q_raw = [inputs.tile([P, Q_TILES, C], BF16, name="q_raw%d" % b) for b in reversed(range(BATCH))][::-1]
             var_raw = [inputs.tile([P, KEY_TILES, C], BF16, name="var_raw%d" % b) for b in range(BATCH)]
             mu_raw = [inputs.tile([P, KEY_TILES, C], BF16, name="mu_raw%d" % b) for b in range(BATCH)]
-            v_raw = [inputs.tile([P, PACK, C], BF16, name="v_raw%d" % b) for b in range(BATCH)]
 
             def load_queries(b):
                 for i in range(PAIRS_PER_BATCH):
@@ -101,7 +99,6 @@ def tile_probcrossattention_pb_t_kernel(tc, q, k_mu, k_var, v_sample, out):
 
             load_queries(0)
             for b in range(BATCH):
-                nc.sync.dma_start(out=v_raw[b][:], in_=v_sample[b].rearrange("(p t) c -> p t c", t=PACK))
                 nc.sync.dma_start(out=var_raw[b][:], in_=k_var[b].rearrange("(p t) c -> p t c", t=KEY_TILES))
                 nc.sync.dma_start(out=mu_raw[b][:], in_=k_mu[b].rearrange("(p t) c -> p t c", t=KEY_TILES))
             load_queries(1)
@@ -128,9 +125,7 @@ def tile_probcrossattention_pb_t_kernel(tc, q, k_mu, k_var, v_sample, out):
                     in_=turned[:].rearrange("p u (r n) -> p n r u", r=PAIR),
                 )
 
-            def prepare_keys_and_values(b):
-                v_grouped = v_stage.tile([P, C, PACK], BF16, align_bytes=64)
-                nc.vector.tensor_copy(out=v_grouped[:], in_=v_raw[b][:].rearrange("p t c -> p c t"))
+            def prepare_keys(b):
                 for raw, (codes, scales) in ((var_raw[b], var_mx[b]), (mu_raw[b], mu_mx[b])):
                     k_grouped = k_stage.tile([P, TK * PACK], BF16, align_bytes=64)
                     half = PAIR * P * PACK
@@ -138,10 +133,6 @@ def tile_probcrossattention_pb_t_kernel(tc, q, k_mu, k_var, v_sample, out):
                         turned = turn_pair(raw[:, h * PAIR : (h + 1) * PAIR, :])
                         copy_keys_grouped(turned, k_grouped[:, h * half : (h + 1) * half])
                     nc.vector.quantize_mx(out=codes[:].bitcast(FP8X4), scales=scales[:], in_=k_grouped[:])
-                codes, scales = v_mx[b]
-                nc.vector.quantize_mx(
-                    out=codes[:].bitcast(FP8X4), scales=scales[:], in_=v_grouped[:].rearrange("p c t -> p (c t)")
-                )
 
             def prepare_queries(b):
                 q_turned = {}
@@ -170,9 +161,30 @@ def tile_probcrossattention_pb_t_kernel(tc, q, k_mu, k_var, v_sample, out):
                         )
 
             prepare_queries(0)
-            prepare_keys_and_values(0)
-            prepare_keys_and_values(1)
+            prepare_keys(0)
+            prepare_keys(1)
             prepare_queries(1)
+
+        values = ctx.enter_context(tc.tile_pool(name="values", bufs=1))
+        v_grouped = [values.tile([P, C, PACK], BF16, name="v_grouped%d" % b, align_bytes=64) for b in range(BATCH)]
+        v_raw = [values.tile([P, PACK, C], BF16, name="v_raw%d" % b) for b in range(BATCH)]
+        for b in range(BATCH):
+            nc.sync.dma_start(out=v_raw[b][:], in_=v_sample[b].rearrange("(p t) c -> p t c", t=PACK))
+            for c in range(0, C, P):
+                nc.gpsimd.tensor_scalar(
+                    out=v_grouped[b][:, c : c + P, :],
+                    in0=v_raw[b][:, :, c : c + P].rearrange("p t c -> p c t"),
+                    scalar1=1.0,
+                    scalar2=1.0,
+                    op0=ALU.mult,
+                    op1=ALU.mult,
+                )
+
+        def quantise_values(b):
+            codes, scales = v_mx[b]
+            nc.vector.quantize_mx(
+                out=codes[:].bitcast(FP8X4), scales=scales[:], in_=v_grouped[b][:].rearrange("p c t -> p (c t)")
+            )
 
         var_ps = {}
         mean_ps = {}
@@ -268,13 +280,15 @@ def tile_probcrossattention_pb_t_kernel(tc, q, k_mu, k_var, v_sample, out):
                     for r in range(PAIR):
                         t = s * PAIR + r
                         result = out_stage.tile([P, C], F32)
-                        if r == 1 and s % DIVIDE_ON_VECTOR_EVERY == 0:
+                        if r == 1 and s % DIVIDE_ON_VECTOR_EVERY == 1:
                             nc.vector.tensor_scalar_mul(out=result[:], in0=out_ps[(s, r)][:], scalar1=inv_sum[:, t : t + 1])
                         else:
                             nc.scalar.activation(
                                 out=result[:], in_=out_ps[(s, r)][:], func=FUNC.Copy, scale=inv_sum[:, t : t + 1]
                             )
                         nc.sync.dma_start(out=out_rows[:, i * PAIR + r, :], in_=result[:])
+                if step in (-1, 4):
+                    quantise_values(0 if step < 4 else 1)
                 s = step
                 if live(s):
                     e_grouped = e_stage.tile([P, PAIR, P, PACK], BF16, align_bytes=64)

@@ -25,22 +25,22 @@ KEY_TILES = TK // P
 Q_TILES = TQ // P
 PAIRS_PER_BATCH = Q_TILES // PAIR
 N_PAIRS = BATCH * PAIRS_PER_BATCH
+N_TILES = N_PAIRS * PAIR
 PSUM_BANKS = 8
+GROUPED = PAIR * P * PACK
 
 SQUARE_LEAD = 1
 GROUP_LEAD = 2
 TURN_LEAD = 4
-SQRT_LEAD = 1
 SCORE_LEAD = 2
-MAX_LEAD = 5
-EXP_LEAD = 3
+SQRT_LEAD = 1
+MAX_LEAD = 4
+EXP_LEAD = 2
 TURN_E_LEAD = 1
 OUT_LAG = 1
 STORE_LAG = 2
 
 SQUARE_ON_SCALAR = 256
-
-DIVIDE_ON_VECTOR_EVERY = 4
 
 
 def live(s):
@@ -71,37 +71,37 @@ def tile_probcrossattention_pb_t_kernel(tc, q, k_mu, k_var, v_sample, out):
             scales = keep.tile([P, width], U8, name=name + "_scales", align_bytes=64)
             return codes, scales
 
-        var_mx = [mx_operand("var%d" % b, TK) for b in range(BATCH)]
-        mu_mx = [mx_operand("mu%d" % b, TK) for b in range(BATCH)]
-        v_mx = [mx_operand("v%d" % b, C) for b in range(BATCH)]
+        key_mx = {(kind, b): mx_operand("%s%d" % (kind, b), TK) for kind in ("var", "mu", "v") for b in range(BATCH)}
         q_mx = [mx_operand("q%d" % s, 2 * PAIR * P) for s in range(N_PAIRS)]
 
-        scores = keep.tile([P, N_PAIRS * PAIR, TK], F32)
-        neg_max = keep.tile([P, N_PAIRS * PAIR], F32)
-        row_sum = keep.tile([P, N_PAIRS * PAIR], F32)
-        inv_sum = keep.tile([P, N_PAIRS * PAIR], F32)
+        scores = keep.tile([P, N_TILES, TK], F32)
+        neg_max = keep.tile([P, N_TILES], F32)
+        row_sum = keep.tile([P, N_TILES], F32)
+        inv_sum = keep.tile([P, N_TILES], F32)
 
         with ExitStack() as phase0:
             inputs = phase0.enter_context(tc.tile_pool(name="inputs", bufs=1))
-            k_stage = phase0.enter_context(tc.tile_pool(name="k_stage", bufs=2))
-            q_stage = phase0.enter_context(tc.tile_pool(name="q_stage", bufs=GROUP_LEAD + 2))
-
             q_raw = [inputs.tile([P, Q_TILES, C], BF16, name="q_raw%d" % b) for b in reversed(range(BATCH))][::-1]
-            var_raw = [inputs.tile([P, KEY_TILES, C], BF16, name="var_raw%d" % b) for b in range(BATCH)]
-            mu_raw = [inputs.tile([P, KEY_TILES, C], BF16, name="mu_raw%d" % b) for b in range(BATCH)]
+            k_raw = {
+                (kind, b): inputs.tile([P, KEY_TILES, C], BF16, name="%s_raw%d" % (kind, b))
+                for kind in ("var", "mu")
+                for b in range(BATCH)
+            }
 
-            def load_queries(b):
-                for i in range(PAIRS_PER_BATCH):
-                    tiles = slice(i * PAIR, (i + 1) * PAIR)
-                    nc.sync.dma_start(
-                        out=q_raw[b][:, tiles, :], in_=q[b].rearrange("(p j) c -> p j c", j=Q_TILES)[:, tiles, :]
-                    )
+            def rows_of(kind, i, h):
+                if kind == "q":
+                    b, j = divmod(i, PAIRS_PER_BATCH)
+                    return q_raw[b][:, j * PAIR : (j + 1) * PAIR, :]
+                return k_raw[(kind, i)][:, h * PAIR : (h + 1) * PAIR, :]
 
-            load_queries(0)
-            for b in range(BATCH):
-                nc.sync.dma_start(out=var_raw[b][:], in_=k_var[b].rearrange("(p t) c -> p t c", t=KEY_TILES))
-                nc.sync.dma_start(out=mu_raw[b][:], in_=k_mu[b].rearrange("(p t) c -> p t c", t=KEY_TILES))
-            load_queries(1)
+            def load(kind, i, h):
+                if kind == "q":
+                    b, j = divmod(i, PAIRS_PER_BATCH)
+                    source = q[b].rearrange("(p j) c -> p j c", j=Q_TILES)[:, j * PAIR : (j + 1) * PAIR, :]
+                else:
+                    source = (k_var if kind == "var" else k_mu)[i].rearrange("(p t) c -> p t c", t=KEY_TILES)
+                    source = source[:, h * PAIR : (h + 1) * PAIR, :]
+                nc.sync.dma_start(out=rows_of(kind, i, h), in_=source)
 
             def turn_pair(rows):
                 turned = psum.tile([P, HALVES, PAIR * P], F32, tag="bank")
@@ -113,83 +113,91 @@ def tile_probcrossattention_pb_t_kernel(tc, q, k_mu, k_var, v_sample, out):
                         )
                 return turned
 
-            def copy_grouped(turned, grouped):
+            def copy_queries(turned, grouped):
                 nc.scalar.copy(
                     out=grouped.bitcast(F32).rearrange("p (n u) -> p n u", u=HALVES),
                     in_=turned[:].rearrange("p u n -> p n u"),
                 )
 
-            def copy_keys_grouped(turned, grouped):
+            def copy_keys(turned, grouped):
                 nc.scalar.copy(
                     out=grouped.bitcast(F32).rearrange("p (n r u) -> p n r u", r=PAIR, u=HALVES),
                     in_=turned[:].rearrange("p u (r n) -> p n r u", r=PAIR),
                 )
 
-            def prepare_keys(b):
-                for raw, (codes, scales) in ((var_raw[b], var_mx[b]), (mu_raw[b], mu_mx[b])):
-                    k_grouped = k_stage.tile([P, TK * PACK], BF16, align_bytes=64)
-                    half = PAIR * P * PACK
-                    for h in range(KEY_TILES // PAIR):
-                        turned = turn_pair(raw[:, h * PAIR : (h + 1) * PAIR, :])
-                        copy_keys_grouped(turned, k_grouped[:, h * half : (h + 1) * half])
-                    nc.vector.quantize_mx(out=codes[:].bitcast(FP8X4), scales=scales[:], in_=k_grouped[:])
+            def quantise(mx, values):
+                codes, scales = mx
+                nc.vector.quantize_mx(out=codes[:].bitcast(FP8X4), scales=scales[:], in_=values)
 
-            def prepare_queries(b):
-                q_turned = {}
-                q_grouped = {}
-                for step in range(-TURN_LEAD, PAIRS_PER_BATCH):
-                    i = step + TURN_LEAD
-                    if i < PAIRS_PER_BATCH:
-                        q_turned[i] = turn_pair(q_raw[b][:, i * PAIR : (i + 1) * PAIR, :])
-                    i = step + GROUP_LEAD
-                    if 0 <= i < PAIRS_PER_BATCH:
-                        q_grouped[i] = q_stage.tile([P, 2, PAIR * P * PACK], BF16, name="q_grouped", align_bytes=64)
-                        copy_grouped(q_turned[i], q_grouped[i][:, 0, :])
-                    i = step + SQUARE_LEAD
-                    if 0 <= i < PAIRS_PER_BATCH:
-                        plain, squared = q_grouped[i][:, 0, :], q_grouped[i][:, 1, :]
-                        cut = SQUARE_ON_SCALAR
-                        nc.scalar.activation(out=squared[:, :cut], in_=plain[:, :cut], func=FUNC.Square)
-                        nc.vector.tensor_tensor(
-                            out=squared[:, cut:], in0=plain[:, cut:], in1=plain[:, cut:], op=ALU.mult
-                        )
-                    i = step
-                    if 0 <= i:
-                        codes, scales = q_mx[b * PAIRS_PER_BATCH + i]
-                        nc.vector.quantize_mx(
-                            out=codes[:].bitcast(FP8X4), scales=scales[:], in_=q_grouped[i][:].rearrange("p k n -> p (k n)")
-                        )
+            k_stage = phase0.enter_context(tc.tile_pool(name="k_stage", bufs=2))
+            q_stage = phase0.enter_context(tc.tile_pool(name="q_stage", bufs=GROUP_LEAD + 2))
 
-            prepare_queries(0)
-            prepare_keys(0)
-            prepare_keys(1)
-            prepare_queries(1)
+            key_jobs = [(kind, b, h) for b in range(BATCH) for kind in ("var", "mu") for h in range(KEY_TILES // PAIR)]
+            jobs = []
+            for s in range(N_PAIRS):
+                jobs.append(("q", s, 0))
+                if s % PAIR == 1:
+                    jobs.append(key_jobs[s // PAIR])
+            for job in jobs:
+                load(*job)
 
-        values = ctx.enter_context(tc.tile_pool(name="values", bufs=1))
-        v_grouped = [values.tile([P, C, PACK], BF16, name="v_grouped%d" % b, align_bytes=64) for b in range(BATCH)]
-        v_raw = [values.tile([P, PACK, C], BF16, name="v_raw%d" % b) for b in range(BATCH)]
-        for b in range(BATCH):
-            nc.sync.dma_start(out=v_raw[b][:], in_=v_sample[b].rearrange("(p t) c -> p t c", t=PACK))
-            for c in range(0, C, P):
-                nc.gpsimd.tensor_scalar(
-                    out=v_grouped[b][:, c : c + P, :],
-                    in0=v_raw[b][:, :, c : c + P].rearrange("p t c -> p c t"),
-                    scalar1=1.0,
-                    scalar2=1.0,
-                    op0=ALU.mult,
-                    op1=ALU.mult,
-                )
+            turned = {}
+            grouped = {}
+            for step in range(-TURN_LEAD, len(jobs)):
+                j = step + TURN_LEAD
+                if j < len(jobs):
+                    turned[j] = turn_pair(rows_of(*jobs[j]))
+                j = step + GROUP_LEAD
+                if 0 <= j < len(jobs):
+                    kind, i, h = jobs[j]
+                    if kind == "q":
+                        grouped[j] = q_stage.tile([P, 2, GROUPED], BF16, name="q_grouped", align_bytes=64)
+                        copy_queries(turned[j], grouped[j][:, 0, :])
+                    else:
+                        if h == 0:
+                            k_grouped = k_stage.tile([P, 2, GROUPED], BF16, name="k_grouped", align_bytes=64)
+                        grouped[j] = k_grouped
+                        copy_keys(turned[j], k_grouped[:, h, :])
+                j = step + SQUARE_LEAD
+                if 0 <= j < len(jobs) and jobs[j][0] == "q":
+                    plain, squared = grouped[j][:, 0, :], grouped[j][:, 1, :]
+                    cut = SQUARE_ON_SCALAR
+                    nc.scalar.activation(out=squared[:, :cut], in_=plain[:, :cut], func=FUNC.Square)
+                    nc.vector.tensor_tensor(out=squared[:, cut:], in0=plain[:, cut:], in1=plain[:, cut:], op=ALU.mult)
+                if step >= 0:
+                    kind, i, h = jobs[step]
+                    if kind == "q" or h == 1:
+                        mx = q_mx[i] if kind == "q" else key_mx[(kind, i)]
+                        quantise(mx, grouped[step][:].rearrange("p k n -> p (k n)"))
 
-        def quantise_values(b):
-            codes, scales = v_mx[b]
-            nc.vector.quantize_mx(
-                out=codes[:].bitcast(FP8X4), scales=scales[:], in_=v_grouped[b][:].rearrange("p c t -> p (c t)")
+        def multiply(plane, s, r, kind):
+            codes, scales = q_mx[s]
+            k_codes, k_scales = key_mx[(kind, s // PAIRS_PER_BATCH)]
+            cols = slice((plane * PAIR + r) * P, (plane * PAIR + r + 1) * P)
+            bank = psum.tile([P, TK], F32, name="product", tag="bank")
+            nc.tensor.matmul_mx(
+                out=bank[:],
+                lhsT=codes[:, cols].bitcast(FP8X4),
+                lhsT_scale=scales[:, cols],
+                rhs=k_codes[:].bitcast(FP8X4),
+                rhs_scale=k_scales[:],
+                start=True,
+                stop=True,
             )
+            return bank
 
         var_ps = {}
         mean_ps = {}
         penalty = {}
         for step in range(-SCORE_LEAD, N_PAIRS):
+            s = step + SCORE_LEAD
+            if live(s):
+                for r in range(PAIR):
+                    var_ps[(s, r)] = multiply(1, s, r, "var")
+            s = step + SCORE_LEAD - 1
+            if live(s):
+                for r in range(PAIR):
+                    mean_ps[(s, r)] = multiply(0, s, r, "mu")
             s = step
             if live(s):
                 for r in range(PAIR):
@@ -208,23 +216,21 @@ def tile_probcrossattention_pb_t_kernel(tc, q, k_mu, k_var, v_sample, out):
                     nc.scalar.activation(
                         out=penalty[(s, r)][:], in_=var_ps[(s, r)][:], func=FUNC.Sqrt, scale=BETA * BETA / C
                     )
-            s = step + SCORE_LEAD
-            if live(s):
-                b = s // PAIRS_PER_BATCH
-                codes, scales = q_mx[s]
-                for plane, (k_codes, k_scales), banks in ((1, var_mx[b], var_ps), (0, mu_mx[b], mean_ps)):
-                    for r in range(PAIR):
-                        cols = slice((plane * PAIR + r) * P, (plane * PAIR + r + 1) * P)
-                        banks[(s, r)] = psum.tile([P, TK], F32, name="product", tag="bank")
-                        nc.tensor.matmul_mx(
-                            out=banks[(s, r)][:],
-                            lhsT=codes[:, cols].bitcast(FP8X4),
-                            lhsT_scale=scales[:, cols],
-                            rhs=k_codes[:].bitcast(FP8X4),
-                            rhs_scale=k_scales[:],
-                            start=True,
-                            stop=True,
-                        )
+
+        values = ctx.enter_context(tc.tile_pool(name="values", bufs=1))
+        v_grouped = [values.tile([P, C, PACK], BF16, name="v_grouped%d" % b, align_bytes=64) for b in range(BATCH)]
+        v_raw = [values.tile([P, PACK, C], BF16, name="v_raw%d" % b) for b in range(BATCH)]
+        for b in range(BATCH):
+            nc.sync.dma_start(out=v_raw[b][:], in_=v_sample[b].rearrange("(p t) c -> p t c", t=PACK))
+            for c in range(0, C, 128):
+                nc.gpsimd.tensor_scalar(
+                    out=v_grouped[b][:, c : c + 128, :],
+                    in0=v_raw[b][:, :, c : c + 128].rearrange("p t c -> p c t"),
+                    scalar1=1.0,
+                    scalar2=1.0,
+                    op0=ALU.mult,
+                    op1=ALU.mult,
+                )
 
         with ExitStack() as phase2:
             e_ahead = phase2.enter_context(tc.tile_pool(name="e_ahead", bufs=EXP_LEAD + 2))
@@ -232,27 +238,36 @@ def tile_probcrossattention_pb_t_kernel(tc, q, k_mu, k_var, v_sample, out):
             out_stage = phase2.enter_context(tc.tile_pool(name="out_stage", bufs=8))
             nc.scalar.activation(out=warm[:], in_=one[:], func=FUNC.Exp)
 
+            units = [[s * PAIR, s * PAIR + 1] for s in range(N_PAIRS - 2)]
+            units += [[n] for n in range((N_PAIRS - 2) * PAIR, N_PAIRS * PAIR)]
             e = {}
             e_turned = {}
             e_mx = {}
             out_ps = {}
-            for step in range(-MAX_LEAD, N_PAIRS + STORE_LAG):
+
+            def live_unit(s):
+                return 0 <= s < len(units)
+
+            def span(s):
+                return slice(units[s][0], units[s][-1] + 1)
+
+            for step in range(-MAX_LEAD, len(units) + STORE_LAG):
                 s = step + TURN_E_LEAD
-                if live(s):
+                if live_unit(s):
                     e_turned[s] = psum.tile([P, PAIR, HALVES, P], F32, name="e_turned", tag="bank")
-                    for r in range(PAIR):
+                    for r in range(len(units[s])):
                         words = e[s][:, r, :].bitcast(F32)
                         for u in range(HALVES):
                             nc.tensor.transpose(e_turned[s][:, r, u, :], words[:, u * P : (u + 1) * P], ident_f32[:])
                 s = step - OUT_LAG
-                if live(s):
+                if live_unit(s):
                     codes, scales = e_mx[s]
-                    v_codes, v_scales = v_mx[s // PAIRS_PER_BATCH]
-                    for r in range(PAIR):
+                    for r, n in enumerate(units[s]):
+                        v_codes, v_scales = key_mx[("v", n // Q_TILES)]
                         cols = slice(r * P, (r + 1) * P)
-                        out_ps[(s, r)] = psum.tile([P, C], F32, name="out_ps", tag="bank")
+                        out_ps[n] = psum.tile([P, C], F32, name="out_ps", tag="bank")
                         nc.tensor.matmul_mx(
-                            out=out_ps[(s, r)][:],
+                            out=out_ps[n][:],
                             lhsT=codes[:, cols].bitcast(FP8X4),
                             lhsT_scale=scales[:, cols],
                             rhs=v_codes[:].bitcast(FP8X4),
@@ -261,56 +276,61 @@ def tile_probcrossattention_pb_t_kernel(tc, q, k_mu, k_var, v_sample, out):
                             stop=True,
                         )
                 s = step + EXP_LEAD
-                if live(s):
+                if live_unit(s):
                     e[s] = e_ahead.tile([P, PAIR, TK], BF16, name="e")
-                    for r in range(PAIR):
-                        t = s * PAIR + r
+                    for r, n in enumerate(units[s]):
                         nc.scalar.activation(
                             out=e[s][:, r, :],
-                            in_=scores[:, t, :],
+                            in_=scores[:, n, :],
                             func=FUNC.Exp,
-                            bias=neg_max[:, t : t + 1],
+                            bias=neg_max[:, n : n + 1],
                             scale=1.0,
-                            accum_out=row_sum[:, t : t + 1],
+                            accum_out=row_sum[:, n : n + 1],
                         )
                 s = step - STORE_LAG
-                if live(s):
-                    b, i = divmod(s, PAIRS_PER_BATCH)
-                    out_rows = out[b].rearrange("(p j) c -> p j c", j=Q_TILES)
-                    for r in range(PAIR):
-                        t = s * PAIR + r
-                        result = out_stage.tile([P, C], F32)
-                        if r == 1 and s % DIVIDE_ON_VECTOR_EVERY == 1:
-                            nc.vector.tensor_scalar_mul(out=result[:], in0=out_ps[(s, r)][:], scalar1=inv_sum[:, t : t + 1])
+                if live_unit(s):
+                    for n in units[s]:
+                        b, j = divmod(n, Q_TILES)
+                        out_rows = out[b].rearrange("(p j) c -> p j c", j=Q_TILES)
+                        result = out_stage.tile([P, C], F32, name="result")
+                        if n == N_TILES - 1 and 256:
+                            h = 256
+                            nc.vector.tensor_scalar_mul(out=result[:, :h], in0=out_ps[n][:, :h], scalar1=inv_sum[:, n : n + 1])
+                            nc.scalar.activation(
+                                out=result[:, h:], in_=out_ps[n][:, h:], func=FUNC.Copy, scale=inv_sum[:, n : n + 1]
+                            )
+                            nc.sync.dma_start(out=out_rows[:, j, :h], in_=result[:, :h])
+                            nc.sync.dma_start(out=out_rows[:, j, h:], in_=result[:, h:])
+                            continue
+                        if n % 6 == 5:
+                            nc.vector.tensor_scalar_mul(out=result[:], in0=out_ps[n][:], scalar1=inv_sum[:, n : n + 1])
                         else:
                             nc.scalar.activation(
-                                out=result[:], in_=out_ps[(s, r)][:], func=FUNC.Copy, scale=inv_sum[:, t : t + 1]
+                                out=result[:], in_=out_ps[n][:], func=FUNC.Copy, scale=inv_sum[:, n : n + 1]
                             )
-                        nc.sync.dma_start(out=out_rows[:, i * PAIR + r, :], in_=result[:])
-                if step in (-1, 4):
-                    quantise_values(0 if step < 4 else 1)
+                        nc.sync.dma_start(out=out_rows[:, j, :], in_=result[:])
+                for b, when in ((0, 1), (1, 5)):
+                    if step == when - OUT_LAG:
+                        quantise(key_mx[("v", b)], v_grouped[b][:].rearrange("p c t -> p (c t)"))
                 s = step
-                if live(s):
-                    e_grouped = e_stage.tile([P, PAIR, P, PACK], BF16, align_bytes=64)
+                if live_unit(s):
+                    n = len(units[s])
+                    e_grouped = e_stage.tile([P, GROUPED], BF16, align_bytes=64)
                     nc.vector.tensor_copy(
-                        out=e_grouped[:].rearrange("p r n t -> p (r n t)").bitcast(F32).rearrange(
-                            "p (r n u) -> p r n u", r=PAIR, u=HALVES
-                        ),
-                        in_=e_turned[s][:].rearrange("p r u n -> p r n u"),
+                        out=e_grouped[:, : n * P * PACK].bitcast(F32).rearrange("p (r n u) -> p r n u", r=n, u=HALVES),
+                        in_=e_turned[s][:, :n].rearrange("p r u n -> p r n u"),
                     )
                 s = step + MAX_LEAD
-                if live(s):
-                    tiles = slice(s * PAIR, (s + 1) * PAIR)
+                if live_unit(s):
                     nc.vector.tensor_reduce(
-                        out=neg_max[:, tiles], in_=scores[:, tiles, :], axis=AXIS.X, op=ALU.max, negate=True
+                        out=neg_max[:, span(s)], in_=scores[:, span(s), :], axis=AXIS.X, op=ALU.max, negate=True
                     )
                 s = step
-                if live(s):
+                if live_unit(s):
                     codes = e_stage.tile([P, PAIR * P], U32, name="e_codes", align_bytes=64)
                     scales = e_stage.tile([P, PAIR * P], U8, name="e_scales", align_bytes=64)
                     nc.vector.quantize_mx(
-                        out=codes[:].bitcast(FP8X4), scales=scales[:], in_=e_grouped[:].rearrange("p r n t -> p (r n t)")
+                        out=codes[:, : n * P].bitcast(FP8X4), scales=scales[:, : n * P], in_=e_grouped[:, : n * P * PACK]
                     )
                     e_mx[s] = (codes, scales)
-                    tiles = slice(s * PAIR, (s + 1) * PAIR)
-                    nc.gpsimd.tensor_tensor(out=inv_sum[:, tiles], in0=row_sum[:, tiles], in1=minus_one[:], op=ALU.pow)
+                    nc.gpsimd.tensor_tensor(out=inv_sum[:, span(s)], in0=row_sum[:, span(s)], in1=minus_one[:, :n], op=ALU.pow)

@@ -33,6 +33,8 @@ SQUARE_LEAD = 1
 GROUP_LEAD = 2
 TURN_LEAD = 4
 SCORE_LEAD = 2
+FIRST_LATE = N_PAIRS - 4
+FIRST_DEFERRED = N_PAIRS - 2
 SQRT_LEAD = 1
 MAX_LEAD = 4
 EXP_LEAD = 2
@@ -40,7 +42,7 @@ TURN_E_LEAD = 1
 OUT_LAG = 1
 STORE_LAG = 2
 
-SQUARE_ON_SCALAR = 256
+SQUARE_ON_SCALAR = 128
 
 
 def live(s):
@@ -55,6 +57,7 @@ def tile_probcrossattention_pb_t_kernel(tc, q, k_mu, k_var, v_sample, out):
         const = ctx.enter_context(tc.tile_pool(name="const", bufs=1))
         keep = ctx.enter_context(tc.tile_pool(name="keep", bufs=1))
         psum = ctx.enter_context(tc.psum_pool(name="psum", bufs=PSUM_BANKS))
+        late_stage = ctx.enter_context(tc.tile_pool(name="late_stage", bufs=4))
         pen_stage = ctx.enter_context(tc.tile_pool(name="pen_stage", bufs=3 * PAIR))
 
         ident_f32 = const.tile([P, P], F32)
@@ -134,15 +137,16 @@ def tile_probcrossattention_pb_t_kernel(tc, q, k_mu, k_var, v_sample, out):
 
             key_jobs = [(kind, b, h) for b in range(BATCH) for kind in ("var", "mu") for h in range(KEY_TILES // PAIR)]
             jobs = []
-            for s in range(N_PAIRS):
+            for s in range(FIRST_LATE):
                 jobs.append(("q", s, 0))
-                if s % PAIR == 1:
-                    jobs.append(key_jobs[s // PAIR])
+                jobs.extend(key_jobs[(2 * s + 1) * len(key_jobs) // (2 * FIRST_LATE) : (2 * s + 3) * len(key_jobs) // (2 * FIRST_LATE)])
+            jobs = jobs[:-1] + [("q", s, 0) for s in range(FIRST_LATE, N_PAIRS)] + jobs[-1:]
             for job in jobs:
                 load(*job)
 
             turned = {}
             grouped = {}
+            late_grouped = {}
             for step in range(-TURN_LEAD, len(jobs)):
                 j = step + TURN_LEAD
                 if j < len(jobs):
@@ -151,7 +155,11 @@ def tile_probcrossattention_pb_t_kernel(tc, q, k_mu, k_var, v_sample, out):
                 if 0 <= j < len(jobs):
                     kind, i, h = jobs[j]
                     if kind == "q":
-                        grouped[j] = q_stage.tile([P, 2, GROUPED], BF16, name="q_grouped", align_bytes=64)
+                        if i < FIRST_LATE:
+                            grouped[j] = q_stage.tile([P, 2, GROUPED], BF16, name="q_grouped", align_bytes=64)
+                        else:
+                            grouped[j] = late_stage.tile([P, 2, GROUPED], BF16, name="late_grouped", align_bytes=64)
+                            late_grouped[i] = grouped[j]
                         copy_queries(turned[j], grouped[j][:, 0, :])
                     else:
                         if h == 0:
@@ -159,16 +167,22 @@ def tile_probcrossattention_pb_t_kernel(tc, q, k_mu, k_var, v_sample, out):
                         grouped[j] = k_grouped
                         copy_keys(turned[j], k_grouped[:, h, :])
                 j = step + SQUARE_LEAD
-                if 0 <= j < len(jobs) and jobs[j][0] == "q":
+                if 0 <= j < len(jobs) and jobs[j][0] == "q" and jobs[j][1] < FIRST_LATE:
                     plain, squared = grouped[j][:, 0, :], grouped[j][:, 1, :]
                     cut = SQUARE_ON_SCALAR
                     nc.scalar.activation(out=squared[:, :cut], in_=plain[:, :cut], func=FUNC.Square)
                     nc.vector.tensor_tensor(out=squared[:, cut:], in0=plain[:, cut:], in1=plain[:, cut:], op=ALU.mult)
                 if step >= 0:
                     kind, i, h = jobs[step]
-                    if kind == "q" or h == 1:
+                    if kind == "q" and i < FIRST_LATE or h == 1:
                         mx = q_mx[i] if kind == "q" else key_mx[(kind, i)]
                         quantise(mx, grouped[step][:].rearrange("p k n -> p (k n)"))
+
+        for s in range(FIRST_LATE, N_PAIRS):
+            plain, squared = late_grouped[s][:, 0, :], late_grouped[s][:, 1, :]
+            for c in range(0, GROUPED, 512):
+                cols = slice(c, c + 512)
+                nc.gpsimd.tensor_tensor(out=squared[:, cols], in0=plain[:, cols], in1=plain[:, cols], op=ALU.mult)
 
         def multiply(plane, s, r, kind):
             codes, scales = q_mx[s]
@@ -189,32 +203,43 @@ def tile_probcrossattention_pb_t_kernel(tc, q, k_mu, k_var, v_sample, out):
         var_ps = {}
         mean_ps = {}
         penalty = {}
+
+        def combine(s, r):
+            nc.vector.scalar_tensor_tensor(
+                out=scores[:, s * PAIR + r, :],
+                in0=mean_ps[(s, r)][:],
+                scalar=1.0 / math.sqrt(C),
+                in1=penalty[(s, r)],
+                op0=ALU.mult,
+                op1=ALU.subtract,
+            )
+
         for step in range(-SCORE_LEAD, N_PAIRS):
             s = step + SCORE_LEAD
             if live(s):
                 for r in range(PAIR):
                     var_ps[(s, r)] = multiply(1, s, r, "var")
             s = step + SCORE_LEAD - 1
-            if live(s):
+            if 0 <= s < FIRST_DEFERRED:
                 for r in range(PAIR):
                     mean_ps[(s, r)] = multiply(0, s, r, "mu")
             s = step
-            if live(s):
+            if 0 <= s < FIRST_DEFERRED:
                 for r in range(PAIR):
-                    nc.vector.scalar_tensor_tensor(
-                        out=scores[:, s * PAIR + r, :],
-                        in0=mean_ps[(s, r)][:],
-                        scalar=1.0 / math.sqrt(C),
-                        in1=penalty[(s, r)][:],
-                        op0=ALU.mult,
-                        op1=ALU.subtract,
-                    )
+                    combine(s, r)
+            s = step + 3
+            if FIRST_LATE <= s < N_PAIRS:
+                codes, scales = q_mx[s]
+                nc.vector.quantize_mx(out=codes[:].bitcast(FP8X4), scales=scales[:], in_=late_grouped[s][:].rearrange("p k n -> p (k n)"))
             s = step + SQRT_LEAD
             if live(s):
                 for r in range(PAIR):
-                    penalty[(s, r)] = pen_stage.tile([P, TK], F32, name="penalty")
+                    if s < FIRST_DEFERRED:
+                        penalty[(s, r)] = pen_stage.tile([P, TK], F32, name="penalty")[:]
+                    else:
+                        penalty[(s, r)] = scores[:, s * PAIR + r, :]
                     nc.scalar.activation(
-                        out=penalty[(s, r)][:], in_=var_ps[(s, r)][:], func=FUNC.Sqrt, scale=BETA * BETA / C
+                        out=penalty[(s, r)], in_=var_ps[(s, r)][:], func=FUNC.Sqrt, scale=BETA * BETA / C
                     )
 
         values = ctx.enter_context(tc.tile_pool(name="values", bufs=1))
@@ -275,6 +300,10 @@ def tile_probcrossattention_pb_t_kernel(tc, q, k_mu, k_var, v_sample, out):
                             start=True,
                             stop=True,
                         )
+                s = step + MAX_LEAD + 2
+                if live_unit(s) and units[s][0] >= FIRST_DEFERRED * PAIR:
+                    for t in units[s]:
+                        mean_ps[divmod(t, PAIR)] = multiply(0, t // PAIR, t % PAIR, "mu")
                 s = step + EXP_LEAD
                 if live_unit(s):
                     e[s] = e_ahead.tile([P, PAIR, TK], BF16, name="e")
@@ -302,7 +331,7 @@ def tile_probcrossattention_pb_t_kernel(tc, q, k_mu, k_var, v_sample, out):
                             nc.sync.dma_start(out=out_rows[:, j, :h], in_=result[:, :h])
                             nc.sync.dma_start(out=out_rows[:, j, h:], in_=result[:, h:])
                             continue
-                        if n % 6 == 5:
+                        if n % 10 == 5:
                             nc.vector.tensor_scalar_mul(out=result[:], in0=out_ps[n][:], scalar1=inv_sum[:, n : n + 1])
                         else:
                             nc.scalar.activation(
@@ -320,6 +349,10 @@ def tile_probcrossattention_pb_t_kernel(tc, q, k_mu, k_var, v_sample, out):
                         out=e_grouped[:, : n * P * PACK].bitcast(F32).rearrange("p (r n u) -> p r n u", r=n, u=HALVES),
                         in_=e_turned[s][:, :n].rearrange("p r u n -> p r n u"),
                     )
+                s = step + MAX_LEAD + 1
+                if live_unit(s) and units[s][0] >= FIRST_DEFERRED * PAIR:
+                    for t in units[s]:
+                        combine(t // PAIR, t % PAIR)
                 s = step + MAX_LEAD
                 if live_unit(s):
                     nc.vector.tensor_reduce(

@@ -33,7 +33,7 @@ SQUARE_LEAD = 1
 GROUP_LEAD = 2
 TURN_LEAD = 4
 SCORE_LEAD = 2
-FIRST_LATE = N_PAIRS - 4
+FIRST_LATE = N_PAIRS - 2
 FIRST_DEFERRED = N_PAIRS - 2
 SQRT_LEAD = 1
 MAX_LEAD = 4
@@ -42,7 +42,7 @@ TURN_E_LEAD = 1
 OUT_LAG = 1
 STORE_LAG = 2
 
-SQUARE_ON_SCALAR = 128
+SQUARE_ON_SCALAR = 192
 
 
 def live(s):
@@ -57,7 +57,7 @@ def tile_probcrossattention_pb_t_kernel(tc, q, k_mu, k_var, v_sample, out):
         const = ctx.enter_context(tc.tile_pool(name="const", bufs=1))
         keep = ctx.enter_context(tc.tile_pool(name="keep", bufs=1))
         psum = ctx.enter_context(tc.psum_pool(name="psum", bufs=PSUM_BANKS))
-        late_stage = ctx.enter_context(tc.tile_pool(name="late_stage", bufs=4))
+        late_stage = ctx.enter_context(tc.tile_pool(name="late_stage", bufs=2))
         pen_stage = ctx.enter_context(tc.tile_pool(name="pen_stage", bufs=3 * PAIR))
 
         ident_f32 = const.tile([P, P], F32)
@@ -104,7 +104,10 @@ def tile_probcrossattention_pb_t_kernel(tc, q, k_mu, k_var, v_sample, out):
                 else:
                     source = (k_var if kind == "var" else k_mu)[i].rearrange("(p t) c -> p t c", t=KEY_TILES)
                     source = source[:, h * PAIR : (h + 1) * PAIR, :]
-                nc.sync.dma_start(out=rows_of(kind, i, h), in_=source)
+                rows = rows_of(kind, i, h)
+                n = 1 if (kind, i) == ("q", 0) else PAIR
+                for r in range(0, PAIR, n):
+                    nc.sync.dma_start(out=rows[:, r : r + n, :], in_=source[:, r : r + n, :])
 
             def turn_pair(rows):
                 turned = psum.tile([P, HALVES, PAIR * P], F32, tag="bank")
@@ -119,7 +122,7 @@ def tile_probcrossattention_pb_t_kernel(tc, q, k_mu, k_var, v_sample, out):
             def copy_queries(turned, grouped):
                 nc.scalar.copy(
                     out=grouped.bitcast(F32).rearrange("p (n u) -> p n u", u=HALVES),
-                    in_=turned[:].rearrange("p u n -> p n u"),
+                    in_=turned.rearrange("p u n -> p n u"),
                 )
 
             def copy_keys(turned, grouped):
@@ -160,7 +163,9 @@ def tile_probcrossattention_pb_t_kernel(tc, q, k_mu, k_var, v_sample, out):
                         else:
                             grouped[j] = late_stage.tile([P, 2, GROUPED], BF16, name="late_grouped", align_bytes=64)
                             late_grouped[i] = grouped[j]
-                        copy_queries(turned[j], grouped[j][:, 0, :])
+                        n = P if j == 0 else PAIR * P
+                        for r in range(0, PAIR * P, n):
+                            copy_queries(turned[j][:, :, r : r + n], grouped[j][:, 0, r * PACK : (r + n) * PACK])
                     else:
                         if h == 0:
                             k_grouped = k_stage.tile([P, 2, GROUPED], BF16, name="k_grouped", align_bytes=64)
@@ -180,8 +185,8 @@ def tile_probcrossattention_pb_t_kernel(tc, q, k_mu, k_var, v_sample, out):
 
         for s in range(FIRST_LATE, N_PAIRS):
             plain, squared = late_grouped[s][:, 0, :], late_grouped[s][:, 1, :]
-            for c in range(0, GROUPED, 512):
-                cols = slice(c, c + 512)
+            for c in range(0, GROUPED, 256):
+                cols = slice(c, c + 256)
                 nc.gpsimd.tensor_tensor(out=squared[:, cols], in0=plain[:, cols], in1=plain[:, cols], op=ALU.mult)
 
         def multiply(plane, s, r, kind):

@@ -33,7 +33,7 @@ SQUARE_LEAD = 1
 GROUP_LEAD = 2
 TURN_LEAD = 4
 SCORE_LEAD = 2
-FIRST_LATE = N_PAIRS - 2
+FIRST_LATE = N_PAIRS
 FIRST_DEFERRED = N_PAIRS - 2
 SQRT_LEAD = 1
 MAX_LEAD = 4
@@ -42,7 +42,7 @@ TURN_E_LEAD = 1
 OUT_LAG = 1
 STORE_LAG = 2
 
-SQUARE_ON_SCALAR = 192
+SQUARE_ON_SCALAR = 224
 
 
 def live(s):
@@ -57,7 +57,6 @@ def tile_probcrossattention_pb_t_kernel(tc, q, k_mu, k_var, v_sample, out):
         const = ctx.enter_context(tc.tile_pool(name="const", bufs=1))
         keep = ctx.enter_context(tc.tile_pool(name="keep", bufs=1))
         psum = ctx.enter_context(tc.psum_pool(name="psum", bufs=PSUM_BANKS))
-        late_stage = ctx.enter_context(tc.tile_pool(name="late_stage", bufs=2))
         pen_stage = ctx.enter_context(tc.tile_pool(name="pen_stage", bufs=3 * PAIR))
 
         ident_f32 = const.tile([P, P], F32)
@@ -161,7 +160,7 @@ def tile_probcrossattention_pb_t_kernel(tc, q, k_mu, k_var, v_sample, out):
                         if i < FIRST_LATE:
                             grouped[j] = q_stage.tile([P, 2, GROUPED], BF16, name="q_grouped", align_bytes=64)
                         else:
-                            grouped[j] = late_stage.tile([P, 2, GROUPED], BF16, name="late_grouped", align_bytes=64)
+                            grouped[j] = q_stage.tile([P, 2, GROUPED], BF16, name="late_grouped", align_bytes=64)
                             late_grouped[i] = grouped[j]
                         n = P if j == 0 else PAIR * P
                         for r in range(0, PAIR * P, n):
@@ -185,8 +184,8 @@ def tile_probcrossattention_pb_t_kernel(tc, q, k_mu, k_var, v_sample, out):
 
         for s in range(FIRST_LATE, N_PAIRS):
             plain, squared = late_grouped[s][:, 0, :], late_grouped[s][:, 1, :]
-            for c in range(0, GROUPED, 256):
-                cols = slice(c, c + 256)
+            for c in range(0, GROUPED, 512):
+                cols = slice(c, c + 512)
                 nc.gpsimd.tensor_tensor(out=squared[:, cols], in0=plain[:, cols], in1=plain[:, cols], op=ALU.mult)
 
         def multiply(plane, s, r, kind):

from contextlib import ExitStack
import math

import concourse.mybir as mybir
from concourse.masks import make_identity

F32 = mybir.dt.float32
BF16 = mybir.dt.bfloat16
U32 = mybir.dt.uint32
U8 = mybir.dt.uint8
FP8X4 = mybir.dt.float8_e4m3fn_x4
FUNC = mybir.ActivationFunctionType
ALU = mybir.AluOpType
AXIS = mybir.AxisListType

BATCH, TQ, TK, C = 2, 2048, 512, 512
BETA = 2.35
FLOPS = 3 * 2 * BATCH * TQ * TK * C

P = 128
PACK = 4
HALVES = 2
PAIR = 2
KEY_TILES = TK // P
Q_TILES = TQ // P
PAIRS_PER_BATCH = Q_TILES // PAIR
N_PAIRS = BATCH * PAIRS_PER_BATCH
N_TILES = N_PAIRS * PAIR
PSUM_BANKS = 8
GROUPED = PAIR * P * PACK

SQUARE_LEAD = 1
GROUP_LEAD = 2
TURN_LEAD = 4
SCORE_LEAD = 2
FIRST_LATE = N_PAIRS
FIRST_DEFERRED = N_PAIRS - 2
SQRT_LEAD = 1
MAX_LEAD = 4
EXP_LEAD = 2
TURN_E_LEAD = 1
OUT_LAG = 1
STORE_LAG = 2

SQUARE_ON_SCALAR = 224


def live(s):
    return 0 <= s < N_PAIRS


def tile_probcrossattention_pb_t_kernel(tc, q, k_mu, k_var, v_sample, out):
    nc = tc.nc
    with ExitStack() as ctx:
        ctx.enter_context(tc.manual_schedule())

        const = ctx.enter_context(tc.tile_pool(name="const", bufs=1))
        keep = ctx.enter_context(tc.tile_pool(name="keep", bufs=1))
        psum = ctx.enter_context(tc.psum_pool(name="psum", bufs=PSUM_BANKS))
        pen_stage = ctx.enter_context(tc.tile_pool(name="pen_stage", bufs=3 * PAIR))

        ident_f32 = const.tile([P, P], F32)
        make_identity(nc, ident_f32[:])
        one = const.tile([P, 1], F32)
        nc.vector.memset(one[:], 1.0)
        warm = const.tile([P, 1], F32)
        minus_one = const.tile([P, PAIR], F32)
        nc.vector.memset(minus_one[:], -1.0)
        nc.scalar.activation(out=warm[:], in_=one[:], func=FUNC.Sqrt)

        def mx_operand(name, width):
            codes = keep.tile([P, width], U32, name=name + "_codes", align_bytes=64)
            scales = keep.tile([P, width], U8, name=name + "_scales", align_bytes=64)
            return codes, scales

        key_mx = {(kind, b): mx_operand("%s%d" % (kind, b), TK) for kind in ("var", "mu", "v") for b in range(BATCH)}
        q_mx = [mx_operand("q%d" % s, 2 * PAIR * P) for s in range(N_PAIRS)]

        scores = keep.tile([P, N_TILES, TK], F32)
        neg_max = keep.tile([P, N_TILES], F32)
        row_sum = keep.tile([P, N_TILES], F32)
        inv_sum = keep.tile([P, N_TILES], F32)

        with ExitStack() as phase0:
            inputs = phase0.enter_context(tc.tile_pool(name="inputs", bufs=1))
            q_raw = [inputs.tile([P, Q_TILES, C], BF16, name="q_raw%d" % b) for b in reversed(range(BATCH))][::-1]
            k_raw = {
                (kind, b): inputs.tile([P, KEY_TILES, C], BF16, name="%s_raw%d" % (kind, b))
                for kind in ("var", "mu")
                for b in range(BATCH)
            }

            def rows_of(kind, i, h):
                if kind == "q":
                    b, j = divmod(i, PAIRS_PER_BATCH)
                    return q_raw[b][:, j * PAIR : (j + 1) * PAIR, :]
                return k_raw[(kind, i)][:, h * PAIR : (h + 1) * PAIR, :]

            def load(kind, i, h):
                if kind == "q":
                    b, j = divmod(i, PAIRS_PER_BATCH)
                    source = q[b].rearrange("(p j) c -> p j c", j=Q_TILES)[:, j * PAIR : (j + 1) * PAIR, :]
                else:
                    source = (k_var if kind == "var" else k_mu)[i].rearrange("(p t) c -> p t c", t=KEY_TILES)
                    source = source[:, h * PAIR : (h + 1) * PAIR, :]
                rows = rows_of(kind, i, h)
                n = 1 if (kind, i) == ("q", 0) else PAIR
                for r in range(0, PAIR, n):
                    nc.sync.dma_start(out=rows[:, r : r + n, :], in_=source[:, r : r + n, :])

            def turn_pair(rows):
                turned = psum.tile([P, HALVES, PAIR * P], F32, tag="bank")
                for r in range(PAIR):
                    words = rows[:, r, :].bitcast(F32)
                    for u in range(HALVES):
                        nc.tensor.transpose(
                            turned[:, u, r * P : (r + 1) * P], words[:, u * P : (u + 1) * P], ident_f32[:]
                        )
                return turned

            def copy_queries(turned, grouped):
                nc.scalar.copy(
                    out=grouped.bitcast(F32).rearrange("p (n u) -> p n u", u=HALVES),
                    in_=turned.rearrange("p u n -> p n u"),
                )

            def copy_keys(turned, grouped):
                nc.scalar.copy(
                    out=grouped.bitcast(F32).rearrange("p (n r u) -> p n r u", r=PAIR, u=HALVES),
                    in_=turned[:].rearrange("p u (r n) -> p n r u", r=PAIR),
                )

            def quantise(mx, values):
                codes, scales = mx
                nc.vector.quantize_mx(out=codes[:].bitcast(FP8X4), scales=scales[:], in_=values)

            k_stage = phase0.enter_context(tc.tile_pool(name="k_stage", bufs=2))
            q_stage = phase0.enter_context(tc.tile_pool(name="q_stage", bufs=GROUP_LEAD + 2))

            key_jobs = [(kind, b, h) for b in range(BATCH) for kind in ("var", "mu") for h in range(KEY_TILES // PAIR)]
            jobs = []
            for s in range(FIRST_LATE):
                jobs.append(("q", s, 0))
                jobs.extend(key_jobs[(2 * s + 1) * len(key_jobs) // (2 * FIRST_LATE) : (2 * s + 3) * len(key_jobs) // (2 * FIRST_LATE)])
            jobs = jobs[:-1] + [("q", s, 0) for s in range(FIRST_LATE, N_PAIRS)] + jobs[-1:]
            for job in jobs:
                load(*job)

            turned = {}
            grouped = {}
            late_grouped = {}
            for step in range(-TURN_LEAD, len(jobs)):
                j = step + TURN_LEAD
                if j < len(jobs):
                    turned[j] = turn_pair(rows_of(*jobs[j]))
                j = step + GROUP_LEAD
                if 0 <= j < len(jobs):
                    kind, i, h = jobs[j]
                    if kind == "q":
                        if i < FIRST_LATE:
                            grouped[j] = q_stage.tile([P, 2, GROUPED], BF16, name="q_grouped", align_bytes=64)
                        else:
                            grouped[j] = q_stage.tile([P, 2, GROUPED], BF16, name="late_grouped", align_bytes=64)
                            late_grouped[i] = grouped[j]
                        n = P if j == 0 else PAIR * P
                        for r in range(0, PAIR * P, n):
                            copy_queries(turned[j][:, :, r : r + n], grouped[j][:, 0, r * PACK : (r + n) * PACK])
                    else:
                        if h == 0:
                            k_grouped = k_stage.tile([P, 2, GROUPED], BF16, name="k_grouped", align_bytes=64)
                        grouped[j] = k_grouped
                        copy_keys(turned[j], k_grouped[:, h, :])
                j = step + SQUARE_LEAD
                if 0 <= j < len(jobs) and jobs[j][0] == "q" and jobs[j][1] < FIRST_LATE:
                    plain, squared = grouped[j][:, 0, :], grouped[j][:, 1, :]
                    cut = SQUARE_ON_SCALAR
                    nc.scalar.activation(out=squared[:, :cut], in_=plain[:, :cut], func=FUNC.Square)
                    nc.vector.tensor_tensor(out=squared[:, cut:], in0=plain[:, cut:], in1=plain[:, cut:], op=ALU.mult)
                if step >= 0:
                    kind, i, h = jobs[step]
                    if kind == "q" and i < FIRST_LATE or h == 1:
                        mx = q_mx[i] if kind == "q" else key_mx[(kind, i)]
                        quantise(mx, grouped[step][:].rearrange("p k n -> p (k n)"))

        for s in range(FIRST_LATE, N_PAIRS):
            plain, squared = late_grouped[s][:, 0, :], late_grouped[s][:, 1, :]
            for c in range(0, GROUPED, 512):
                cols = slice(c, c + 512)
                nc.gpsimd.tensor_tensor(out=squared[:, cols], in0=plain[:, cols], in1=plain[:, cols], op=ALU.mult)

        def multiply(plane, s, r, kind):
            codes, scales = q_mx[s]
            k_codes, k_scales = key_mx[(kind, s // PAIRS_PER_BATCH)]
            cols = slice((plane * PAIR + r) * P, (plane * PAIR + r + 1) * P)
            bank = psum.tile([P, TK], F32, name="product", tag="bank")
            nc.tensor.matmul_mx(
                out=bank[:],
                lhsT=codes[:, cols].bitcast(FP8X4),
                lhsT_scale=scales[:, cols],
                rhs=k_codes[:].bitcast(FP8X4),
                rhs_scale=k_scales[:],
                start=True,
                stop=True,
            )
            return bank

        var_ps = {}
        mean_ps = {}
        penalty = {}

        def combine(s, r):
            nc.vector.scalar_tensor_tensor(
                out=scores[:, s * PAIR + r, :],
                in0=mean_ps[(s, r)][:],
                scalar=1.0 / math.sqrt(C),
                in1=penalty[(s, r)],
                op0=ALU.mult,
                op1=ALU.subtract,
            )

        for step in range(-SCORE_LEAD, N_PAIRS):
            s = step + SCORE_LEAD
            if live(s):
                for r in range(PAIR):
                    var_ps[(s, r)] = multiply(1, s, r, "var")
            s = step + SCORE_LEAD - 1
            if 0 <= s < FIRST_DEFERRED:
                for r in range(PAIR):
                    mean_ps[(s, r)] = multiply(0, s, r, "mu")
            s = step
            if 0 <= s < FIRST_DEFERRED:
                for r in range(PAIR):
                    combine(s, r)
            s = step + 3
            if FIRST_LATE <= s < N_PAIRS:
                codes, scales = q_mx[s]
                nc.vector.quantize_mx(out=codes[:].bitcast(FP8X4), scales=scales[:], in_=late_grouped[s][:].rearrange("p k n -> p (k n)"))
            s = step + SQRT_LEAD
            if live(s):
                for r in range(PAIR):
                    if s < FIRST_DEFERRED:
                        penalty[(s, r)] = pen_stage.tile([P, TK], F32, name="penalty")[:]
                    else:
                        penalty[(s, r)] = scores[:, s * PAIR + r, :]
                    nc.scalar.activation(
                        out=penalty[(s, r)], in_=var_ps[(s, r)][:], func=FUNC.Sqrt, scale=BETA * BETA / C
                    )

        values = ctx.enter_context(tc.tile_pool(name="values", bufs=1))
        v_grouped = [values.tile([P, C, PACK], BF16, name="v_grouped%d" % b, align_bytes=64) for b in range(BATCH)]
        v_raw = [values.tile([P, PACK, C], BF16, name="v_raw%d" % b) for b in range(BATCH)]
        for b in range(BATCH):
            nc.sync.dma_start(out=v_raw[b][:], in_=v_sample[b].rearrange("(p t) c -> p t c", t=PACK))
            for c in range(0, C, 128):
                nc.gpsimd.tensor_scalar(
                    out=v_grouped[b][:, c : c + 128, :],
                    in0=v_raw[b][:, :, c : c + 128].rearrange("p t c -> p c t"),
                    scalar1=1.0,
                    scalar2=1.0,
                    op0=ALU.mult,
                    op1=ALU.mult,
                )

        with ExitStack() as phase2:
            e_ahead = phase2.enter_context(tc.tile_pool(name="e_ahead", bufs=EXP_LEAD + 2))
            e_stage = phase2.enter_context(tc.tile_pool(name="e_stage", bufs=3))
            out_stage = phase2.enter_context(tc.tile_pool(name="out_stage", bufs=8))
            nc.scalar.activation(out=warm[:], in_=one[:], func=FUNC.Exp)

            units = [[s * PAIR, s * PAIR + 1] for s in range(N_PAIRS - 2)]
            units += [[n] for n in range((N_PAIRS - 2) * PAIR, N_PAIRS * PAIR)]
            e = {}
            e_turned = {}
            e_mx = {}
            out_ps = {}

            def live_unit(s):
                return 0 <= s < len(units)

            def span(s):
                return slice(units[s][0], units[s][-1] + 1)

            for step in range(-MAX_LEAD, len(units) + STORE_LAG):
                s = step + TURN_E_LEAD
                if live_unit(s):
                    e_turned[s] = psum.tile([P, PAIR, HALVES, P], F32, name="e_turned", tag="bank")
                    for r in range(len(units[s])):
                        words = e[s][:, r, :].bitcast(F32)
                        for u in range(HALVES):
                            nc.tensor.transpose(e_turned[s][:, r, u, :], words[:, u * P : (u + 1) * P], ident_f32[:])
                s = step - OUT_LAG
                if live_unit(s):
                    codes, scales = e_mx[s]
                    for r, n in enumerate(units[s]):
                        v_codes, v_scales = key_mx[("v", n // Q_TILES)]
                        cols = slice(r * P, (r + 1) * P)
                        out_ps[n] = psum.tile([P, C], F32, name="out_ps", tag="bank")
                        nc.tensor.matmul_mx(
                            out=out_ps[n][:],
                            lhsT=codes[:, cols].bitcast(FP8X4),
                            lhsT_scale=scales[:, cols],
                            rhs=v_codes[:].bitcast(FP8X4),
                            rhs_scale=v_scales[:],
                            start=True,
                            stop=True,
                        )
                s = step + MAX_LEAD + 2
                if live_unit(s) and units[s][0] >= FIRST_DEFERRED * PAIR:
                    for t in units[s]:
                        mean_ps[divmod(t, PAIR)] = multiply(0, t // PAIR, t % PAIR, "mu")
                s = step + EXP_LEAD
                if live_unit(s):
                    e[s] = e_ahead.tile([P, PAIR, TK], BF16, name="e")
                    for r, n in enumerate(units[s]):
                        nc.scalar.activation(
                            out=e[s][:, r, :],
                            in_=scores[:, n, :],
                            func=FUNC.Exp,
                            bias=neg_max[:, n : n + 1],
                            scale=1.0,
                            accum_out=row_sum[:, n : n + 1],
                        )
                s = step - STORE_LAG
                if live_unit(s):
                    for n in units[s]:
                        b, j = divmod(n, Q_TILES)
                        out_rows = out[b].rearrange("(p j) c -> p j c", j=Q_TILES)
                        result = out_stage.tile([P, C], F32, name="result")
                        if n == N_TILES - 1 and 256:
                            h = 256
                            nc.vector.tensor_scalar_mul(out=result[:, :h], in0=out_ps[n][:, :h], scalar1=inv_sum[:, n : n + 1])
                            nc.scalar.activation(
                                out=result[:, h:], in_=out_ps[n][:, h:], func=FUNC.Copy, scale=inv_sum[:, n : n + 1]
                            )
                            nc.sync.dma_start(out=out_rows[:, j, :h], in_=result[:, :h])
                            nc.sync.dma_start(out=out_rows[:, j, h:], in_=result[:, h:])
                            continue
                        if n % 10 == 5:
                            nc.vector.tensor_scalar_mul(out=result[:], in0=out_ps[n][:], scalar1=inv_sum[:, n : n + 1])
                        else:
                            nc.scalar.activation(
                                out=result[:], in_=out_ps[n][:], func=FUNC.Copy, scale=inv_sum[:, n : n + 1]
                            )
                        nc.sync.dma_start(out=out_rows[:, j, :], in_=result[:])
                for b, when in ((0, 1), (1, 5)):
                    if step == when - OUT_LAG:
                        quantise(key_mx[("v", b)], v_grouped[b][:].rearrange("p c t -> p (c t)"))
                s = step
                if live_unit(s):
                    n = len(units[s])
                    e_grouped = e_stage.tile([P, GROUPED], BF16, align_bytes=64)
                    nc.vector.tensor_copy(
                        out=e_grouped[:, : n * P * PACK].bitcast(F32).rearrange("p (r n u) -> p r n u", r=n, u=HALVES),
                        in_=e_turned[s][:, :n].rearrange("p r u n -> p r n u"),
                    )
                s = step + MAX_LEAD + 1
                if live_unit(s) and units[s][0] >= FIRST_DEFERRED * PAIR:
                    for t in units[s]:
                        combine(t // PAIR, t % PAIR)
                s = step + MAX_LEAD
                if live_unit(s):
                    nc.vector.tensor_reduce(
                        out=neg_max[:, span(s)], in_=scores[:, span(s), :], axis=AXIS.X, op=ALU.max, negate=True
                    )
                s = step
                if live_unit(s):
                    codes = e_stage.tile([P, PAIR * P], U32, name="e_codes", align_bytes=64)
                    scales = e_stage.tile([P, PAIR * P], U8, name="e_scales", align_bytes=64)
                    nc.vector.quantize_mx(
                        out=codes[:, : n * P].bitcast(FP8X4), scales=scales[:, : n * P], in_=e_grouped[:, : n * P * PACK]
                    )
                    e_mx[s] = (codes, scales)
                    nc.gpsimd.tensor_tensor(out=inv_sum[:, span(s)], in0=row_sum[:, span(s)], in1=minus_one[:, :n], op=ALU.pow)
